import numpy as np
import ml_dtypes


def mxq(x, axis, fmt="e4m3"):
    dtype, down = {"e4m3": (ml_dtypes.float8_e4m3fn, 7), "e5m2": (ml_dtypes.float8_e5m2, 14)}[fmt]
    v = np.moveaxis(np.asarray(x, np.float32).astype(ml_dtypes.bfloat16).astype(np.float64), axis, -1)
    blocks = v.reshape(v.shape[:-1] + (-1, 32))
    amax = np.abs(blocks).max(-1, keepdims=True)
    byte = np.maximum(np.where(amax > 0, np.frexp(amax)[1] - 1 + 127, 0) - down, 1)
    scale = np.exp2(byte - 127.0)
    codes = (blocks / scale).astype(np.float32).astype(dtype).astype(np.float64)
    return np.moveaxis((codes * scale).reshape(v.shape), -1, axis)


WIDE = False


def mx_kscale(k):
    if not WIDE:
        return np.ones(k)
    levels = np.array([10, -10, 5, -5, 0])
    if k % 512:
        return np.exp2(np.random.permutation(np.resize(levels, k // 32))).repeat(32)
    a = np.empty((k // 512, 16))
    for p in range(k // 512):
        a[p, :8] = np.random.permutation(np.resize(levels, 8))
        for g in range(8):
            far = levels[np.abs(levels - a[p, g]) >= 10]
            a[p, g + 8] = far[np.random.randint(len(far))]
    return np.exp2(a.ravel()).repeat(32)


BF16 = ml_dtypes.bfloat16


def bf(x):
    return np.asarray(x, np.float32).astype(BF16)


def f64(x):
    return np.asarray(x).astype(np.float64)


N, G, GIN, GOUT = 1024, 8, 512, 512

P0 = np.array([0.5, 1.0, 0.5, 0.3])
Q0 = np.array([0.5, 0.3, 0.2])


def rational(y, p, q):
    p = p[None, :, :, None]
    q = q[None, :, :, None]
    y2 = y * y
    y3 = y2 * y
    num = p[:, :, 0] + p[:, :, 1] * y + p[:, :, 2] * y2 + p[:, :, 3] * y3
    den = 1.0 + np.abs(q[:, :, 0] * y + q[:, :, 1] * y2 + q[:, :, 2] * y3)
    return num / den


def setup_inputs():
    s = mx_kscale(GIN)
    return {"x": bf(np.random.standard_normal((N, G * GIN)) * np.tile(s, G)),
            "W": bf(np.random.standard_normal((G, GIN, GOUT)) / np.sqrt(GIN) / s[None, :, None]),
            "b": bf(np.random.standard_normal((G, GOUT)) * 0.3),
            "p": bf(P0 + 0.1 * np.random.standard_normal((G, P0.size))),
            "q": bf(Q0 + 0.05 * np.random.standard_normal((G, Q0.size)))}


def core(x, W, b, p, q):
    n = x.shape[0]
    xg = f64(x).reshape(n, G, GIN)
    xq = mxq(xg, 2, "e4m3")
    wq = mxq(f64(W), 1, "e4m3")
    y = (xq.transpose(1, 0, 2) @ wq).transpose(1, 0, 2) + f64(b)[None]
    out = rational(y, f64(p), f64(q))
    return out.reshape(n, G * GOUT)


def e4m3fn_bytes(y):
    return np.clip(np.asarray(y, np.float64), -448.0, 448.0).astype(np.float32).astype(ml_dtypes.float8_e4m3fn).view(np.uint8)


Y_SCALE = 310.0


def reference(x, W, b, p, q):
    out = core(x, W, b, p, q)
    return out, e4m3fn_bytes(out * Y_SCALE)

@@ -1,0 +1,319 @@
+from contextlib import ExitStack
+
+import concourse.masks as masks
+import concourse.mybir as mybir
+
+N_TOK, G, GIN, GOUT = 1024, 8, 512, 512
+FLOPS = 2 * N_TOK * G * GIN * GOUT
+Y_SCALE = 310.0
+
+F32 = mybir.dt.float32
+BF16 = mybir.dt.bfloat16
+U32 = mybir.dt.uint32
+U8 = mybir.dt.uint8
+FP8X4 = mybir.dt.float8_e4m3fn_x4
+FP8 = mybir.dt.float8_e4m3fn
+ACT = mybir.ActivationFunctionType
+ALU = mybir.AluOpType
+
+P = 128
+HALF = 512
+N_HALF = N_TOK // HALF
+T_IN_HALF = HALF // P
+C_TILES = GOUT // P
+N_IDX = G * N_HALF
+N_UNITS = N_IDX * C_TILES
+
+
+def tile_groupkanlayer_kernel(tc, x, W, b, p, q, out_0, out_1):
+    nc = tc.nc
+    with ExitStack() as ctx:
+        const = ctx.enter_context(tc.tile_pool(name="const", bufs=1))
+        raw = ctx.enter_context(tc.tile_pool(name="raw", bufs=1))
+        stage = ctx.enter_context(tc.tile_pool(name="stage", bufs=2))
+        work = ctx.enter_context(tc.tile_pool(name="work", bufs=3))
+        outs = ctx.enter_context(tc.tile_pool(name="outs", bufs=3))
+        ps_x = ctx.enter_context(tc.psum_pool(name="ps_x", bufs=1))
+        ps_acc = ctx.enter_context(tc.psum_pool(name="ps_acc", bufs=3))
+        ps_y = ctx.enter_context(tc.psum_pool(name="ps_y", bufs=2))
+        ps_r = ctx.enter_context(tc.psum_pool(name="ps_r", bufs=2))
+        ctx.enter_context(tc.manual_schedule())
+
+        one_col = const.tile([P, 1], F32, name="one_col")
+        nc.vector.memset(one_col[:], 1.0)
+        warm = const.tile([P, 1], F32, name="warm")
+        nc.scalar.activation(out=warm[:], in_=one_col[:], func=ACT.Abs_reciprocal_sqrt)
+
+        b_rows = const.tile([P, P], BF16, name="b_rows")
+        nc.vector.memset(b_rows[:], 0.0)
+        nc.scalar.dma_start(out=b_rows[0 : G * C_TILES, :], in_=b.rearrange("g (c n) -> (g c) n", n=P))
+        pq_bf = const.tile([P, 56], BF16, name="pq_bf")
+        nc.scalar.dma_start(out=pq_bf[:, 0:32], in_=p.rearrange("g k -> (g k)").partition_broadcast(P))
+        nc.scalar.dma_start(out=pq_bf[:, 32:56], in_=q.rearrange("g k -> (g k)").partition_broadcast(P))
+
+        w_raw = []
+        x_raw = []
+        for g in range(G):
+            wr = raw.tile([P, 4, GOUT], BF16, name="w_raw%d" % g)
+            nc.sync.dma_start(out=wr[:], in_=W[g, :, :].rearrange("(p j) o -> p j o", j=4))
+            w_raw.append(wr)
+            for h in range(N_HALF):
+                xr = raw.tile([P, T_IN_HALF, GIN], BF16, name="x_raw%d_%d" % (g, h))
+                nc.sync.dma_start(
+                    out=xr[:],
+                    in_=x[h * HALF : (h + 1) * HALF, g * GIN : (g + 1) * GIN].rearrange("(t p) k -> p t k", p=P),
+                )
+                x_raw.append(xr)
+
+        ident = const.tile([P, P], F32, name="ident")
+        masks.make_identity(nc, ident[:])
+
+        b_rows32 = const.tile([P, P], F32, name="b_rows32")
+        nc.vector.tensor_copy(out=b_rows32[:], in_=b_rows[:])
+        b_ps = ps_x.tile([P, P], F32, name="b_ps", tag="xt")
+        nc.tensor.transpose(out=b_ps[:], in_=b_rows32[:], identity=ident[:])
+        b_col = const.tile([P, G * C_TILES], F32, name="b_col")
+        nc.vector.tensor_copy(out=b_col[:], in_=b_ps[:, 0 : G * C_TILES])
+        pq = const.tile([P, 56], F32, name="pq")
+        nc.vector.tensor_copy(out=pq[:], in_=pq_bf[:])
+
+        def pcol(g, i):
+            return pq[:, 4 * g + i : 4 * g + i + 1]
+
+        def qcol(g, i):
+            return pq[:, 32 + 3 * g + i : 32 + 3 * g + i + 1]
+
+        wst = {}
+        xst = {}
+        ust = {}
+        ost = {}
+
+        def w_interleave(g, piece):
+            if piece == 0:
+                wst[g] = {"grp": stage.tile([P, GOUT, 4], BF16, name="w_grp", align_bytes=64)}
+            cs = slice(piece * P, (piece + 1) * P)
+            nc.gpsimd.tensor_scalar(
+                out=wst[g]["grp"][:, cs, :],
+                in0=w_raw[g][:, :, cs].rearrange("p j o -> p o j"),
+                scalar1=1.0,
+                scalar2=0.0,
+                op0=ALU.mult,
+                op1=ALU.add,
+            )
+
+        def w_quantize(g):
+            wc = stage.tile([P, GOUT], U32, name="w_codes", align_bytes=64)
+            ws = stage.tile([P, GOUT], U8, name="w_scales", align_bytes=64)
+            nc.vector.quantize_mx(out=wc[:].bitcast(FP8X4), scales=ws[:], in_=wst[g]["grp"][:].rearrange("p o j -> p (o j)"))
+            wst[g]["codes"] = wc
+            wst[g]["scales"] = ws
+
+        def x_transpose(j, a):
+            if a == 0:
+                xst[j] = {"grp": stage.tile([P, HALF * 4], BF16, name="x_grp", align_bytes=64)}
+            xw = x_raw[j][:].bitcast(F32)
+            xt = ps_x.tile([P, 2, 2, P], F32, name="xt", tag="xt")
+            for tt in range(2):
+                for u in range(2):
+                    nc.tensor.transpose(out=xt[:, tt, u, :], in_=xw[:, 2 * a + tt, u : GIN // 2 : 2], identity=ident[:])
+            xst[j]["xt"] = xt
+
+        def x_copy(j, a):
+            dst = xst[j]["grp"][:].bitcast(F32)[:, a * 512 : (a + 1) * 512].rearrange("p (t r u) -> p t r u", t=2, u=2)
+            src = xst[j]["xt"][:].rearrange("p t u r -> p t r u")
+            if a == 0:
+                nc.scalar.copy(out=dst, in_=src)
+            else:
+                nc.vector.tensor_copy(out=dst, in_=src)
+
+        def x_quantize(j):
+            xc = stage.tile([P, HALF], U32, name="x_codes", align_bytes=64)
+            xs = stage.tile([P, HALF], U8, name="x_scales", align_bytes=64)
+            nc.vector.quantize_mx(out=xc[:].bitcast(FP8X4), scales=xs[:], in_=xst[j]["grp"][:])
+            xst[j]["codes"] = xc
+            xst[j]["scales"] = xs
+
+        def ok(u):
+            return 0 <= u < N_UNITS
+
+        def parts(u):
+            j, c = divmod(u, C_TILES)
+            return j // N_HALF, j, c
+
+        def bias_of(u):
+            g, j, c = parts(u)
+            return b_col[:, g * C_TILES + c : g * C_TILES + c + 1]
+
+        def mm(u):
+            g, j, c = parts(u)
+            cs = slice(c * P, (c + 1) * P)
+            acc = ps_acc.tile([P, HALF], F32, name="acc")
+            nc.tensor.matmul_mx(
+                out=acc[:],
+                lhsT=wst[g]["codes"][:, cs].bitcast(FP8X4),
+                lhsT_scale=wst[g]["scales"][:, cs],
+                rhs=xst[j]["codes"][:].bitcast(FP8X4),
+                rhs_scale=xst[j]["scales"][:],
+                start=True,
+                stop=True,
+            )
+            ust[u] = {"acc": acc}
+
+        def s1(u):
+            y_t = work.tile([P, HALF], F32, name="y_t")
+            nc.scalar.activation(out=y_t[:], in_=ust[u]["acc"][:], func=ACT.Identity, bias=bias_of(u), scale=1.0)
+            ust[u]["y_t"] = y_t
+
+        def g1(u):
+            g = parts(u)[0]
+            d_t = work.tile([P, HALF], F32, name="d_t")
+            nc.gpsimd.tensor_scalar(out=d_t[:], in0=ust[u]["y_t"][:], scalar1=qcol(g, 2), scalar2=qcol(g, 1), op0=ALU.mult, op1=ALU.add)
+            ust[u]["d_t"] = d_t
+
+        def v1(u):
+            e_t = work.tile([P, HALF], F32, name="e_t")
+            nc.vector.scalar_tensor_tensor(out=e_t[:], in0=ust[u]["acc"][:], scalar=bias_of(u), in1=ust[u]["d_t"][:], op0=ALU.add, op1=ALU.mult)
+            ust[u]["e_t"] = e_t
+
+        def g2(u):
+            g = parts(u)[0]
+            e2_t = work.tile([P, HALF], F32, name="e2_t")
+            nc.gpsimd.tensor_scalar(out=e2_t[:], in0=ust[u]["e_t"][:], scalar1=one_col[:, 0:1], scalar2=qcol(g, 0), op0=ALU.mult, op1=ALU.add)
+            ust[u]["e2_t"] = e2_t
+
+        def v2(u):
+            f_t = work.tile([P, HALF], F32, name="f_t")
+            nc.vector.scalar_tensor_tensor(out=f_t[:], in0=ust[u]["acc"][:], scalar=bias_of(u), in1=ust[u]["e2_t"][:], op0=ALU.add, op1=ALU.mult)
+            ust[u]["f_t"] = f_t
+
+        def s2(u):
+            af_t = work.tile([P, HALF], F32, name="af_t")
+            nc.scalar.activation(out=af_t[:], in_=ust[u]["f_t"][:], func=ACT.Abs)
+            ust[u]["af_t"] = af_t
+
+        def s3(u):
+            rs_t = work.tile([P, HALF], F32, name="rs_t")
+            nc.scalar.activation(out=rs_t[:], in_=ust[u]["af_t"][:], func=ACT.Abs_reciprocal_sqrt, bias=one_col[:, 0:1], scale=1.0)
+            ust[u]["rs_t"] = rs_t
+
+        def g3(u):
+            r_t = work.tile([P, HALF], F32, name="r_t")
+            nc.gpsimd.tensor_tensor(out=r_t[:], in0=ust[u]["rs_t"][:], in1=ust[u]["rs_t"][:], op=ALU.mult)
+            ust[u]["r_t"] = r_t
+
+        def t_y(u):
+            yb = ps_y.tile([P, T_IN_HALF, P], F32, name="yb")
+            for t in range(T_IN_HALF):
+                nc.tensor.transpose(out=yb[:, t, :], in_=ust[u]["y_t"][:, t * P : (t + 1) * P], identity=ident[:])
+            ust[u]["yb"] = yb
+
+        def t_r(u):
+            rb = ps_r.tile([P, T_IN_HALF, P], F32, name="rb")
+            for t in range(T_IN_HALF):
+                nc.tensor.transpose(out=rb[:, t, :], in_=ust[u]["r_t"][:, t * P : (t + 1) * P], identity=ident[:])
+            ust[u]["rb"] = rb
+
+        def s4(u):
+            g = parts(u)[0]
+            a_d = work.tile([P, HALF], F32, name="a_d")
+            nc.scalar.activation(out=a_d[:], in_=ust[u]["yb"][:].rearrange("p t n -> p (t n)"), func=ACT.Identity, bias=pcol(g, 2), scale=pcol(g, 3))
+            ust[u]["a_d"] = a_d
+
+        def v3(u):
+            b_d = work.tile([P, HALF], F32, name="b_d")
+            nc.vector.tensor_tensor(out=b_d[:], in0=ust[u]["a_d"][:], in1=ust[u]["yb"][:].rearrange("p t n -> p (t n)"), op=ALU.mult)
+            ust[u]["b_d"] = b_d
+
+        def v4(u):
+            g = parts(u)[0]
+            c_d = work.tile([P, T_IN_HALF, P], F32, name="c_d")
+            nc.vector.scalar_tensor_tensor(
+                out=c_d[:].rearrange("p t n -> p (t n)"),
+                in0=ust[u]["b_d"][:],
+                scalar=pcol(g, 1),
+                in1=ust[u]["yb"][:].rearrange("p t n -> p (t n)"),
+                op0=ALU.add,
+                op1=ALU.mult,
+            )
+            ust[u]["c_d"] = c_d
+
+        def v5(u):
+            g, j, c = parts(u)
+            if c == 0:
+                ost[j] = {"o0": outs.tile([P, T_IN_HALF, GOUT], F32, name="o0")}
+            nc.vector.scalar_tensor_tensor(
+                out=ost[j]["o0"][:, :, c * P : (c + 1) * P],
+                in0=ust[u]["c_d"][:],
+                scalar=pcol(g, 0),
+                in1=ust[u]["rb"][:],
+                op0=ALU.add,
+                op1=ALU.mult,
+            )
+
+        def hbm_view(dram, j):
+            g, h = divmod(j, N_HALF)
+            return dram[h * HALF : (h + 1) * HALF, g * GOUT : (g + 1) * GOUT].rearrange("(t p) n -> p t n", p=P)
+
+        def cast(j, t):
+            if t == 0:
+                ost[j]["o1"] = outs.tile([P, T_IN_HALF, GOUT], FP8, name="o1")
+            nc.scalar.activation(out=ost[j]["o1"][:, t, :], in_=ost[j]["o0"][:, t, :], func=ACT.Copy, scale=Y_SCALE, saturate=False)
+
+        for piece in range(C_TILES):
+            w_interleave(0, piece)
+        for a in range(2):
+            x_transpose(0, a)
+            x_copy(0, a)
+        w_quantize(0)
+        x_quantize(0)
+
+        V5_LAG = 4
+        for k in range(-1, N_UNITS + V5_LAG + T_IN_HALF + 1):
+            if ok(k + 1):
+                mm(k + 1)
+            if ok(k - V5_LAG):
+                v5(k - V5_LAG)
+                if (k - V5_LAG) % C_TILES == C_TILES - 1:
+                    jd = (k - V5_LAG) // C_TILES
+                    nc.sync.dma_start(out=hbm_view(out_0, jd), in_=ost[jd]["o0"][:])
+            if ok(k - 1):
+                g2(k - 1)
+                s4(k - 1)
+            if ok(k):
+                t_y(k)
+            if ok(k + 1):
+                s1(k + 1)
+            if ok(k - 1):
+                v2(k - 1)
+            if ok(k):
+                g1(k)
+            if ok(k - 1):
+                v3(k - 1)
+            kc = k - V5_LAG - C_TILES
+            if 0 <= kc < N_UNITS:
+                cast(kc // C_TILES, kc % C_TILES)
+                if kc % C_TILES == C_TILES - 1:
+                    nc.sync.dma_start(out=hbm_view(out_1, kc // C_TILES), in_=ost[kc // C_TILES]["o1"][:].bitcast(U8))
+            if (k + 5) % 4 == 0 and 1 <= (k + 5) // 4 < N_IDX:
+                x_transpose((k + 5) // 4, 0)
+                x_copy((k + 5) // 4, 0)
+            if (k + 4) % 4 == 0 and 1 <= (k + 4) // 4 < N_IDX:
+                x_transpose((k + 4) // 4, 1)
+                x_copy((k + 4) // 4, 1)
+            if ok(k):
+                v1(k)
+            if ok(k - 1):
+                s2(k - 1)
+                s3(k - 1)
+            if ok(k - 2):
+                g3(k - 2)
+            if ok(k - 1):
+                v4(k - 1)
+            if ok(k - 2):
+                t_r(k - 2)
+            if (k + 3) % 4 == 0 and 1 <= (k + 3) // 4 < N_IDX:
+                x_quantize((k + 3) // 4)
+            if k >= 0 and k % 8 < 4 and k // 8 + 1 < G:
+                w_interleave(k // 8 + 1, k % 8)
+            if k >= 0 and k % 8 == 4 and k // 8 + 1 < G:
+                w_quantize(k // 8 + 1)

@@ -39,10 +39,8 @@ def tile_groupkanlayer_kernel(tc, x, W, b, p, q, out_0, out_1):
         ps_r = ctx.enter_context(tc.psum_pool(name="ps_r", bufs=2))
         ctx.enter_context(tc.manual_schedule())
 
-        one_col = const.tile([P, 1], F32, name="one_col")
-        nc.vector.memset(one_col[:], 1.0)
-        warm = const.tile([P, 1], F32, name="warm")
-        nc.scalar.activation(out=warm[:], in_=one_col[:], func=ACT.Abs_reciprocal_sqrt)
+        ident = const.tile([P, P], F32, name="ident")
+        masks.make_identity(nc, ident[:])
 
         b_rows = const.tile([P, P], BF16, name="b_rows")
         nc.vector.memset(b_rows[:], 0.0)
@@ -50,32 +48,35 @@ def tile_groupkanlayer_kernel(tc, x, W, b, p, q, out_0, out_1):
         pq_bf = const.tile([P, 56], BF16, name="pq_bf")
         nc.scalar.dma_start(out=pq_bf[:, 0:32], in_=p.rearrange("g k -> (g k)").partition_broadcast(P))
         nc.scalar.dma_start(out=pq_bf[:, 32:56], in_=q.rearrange("g k -> (g k)").partition_broadcast(P))
+        one_col = const.tile([P, 1], F32, name="one_col")
+        nc.vector.memset(one_col[:], 1.0)
+        warm = const.tile([P, 1], F32, name="warm")
+        nc.scalar.activation(out=warm[:], in_=one_col[:], func=ACT.Abs_reciprocal_sqrt)
 
         w_raw = []
         x_raw = []
         for g in range(G):
-            wr = raw.tile([P, 4, GOUT], BF16, name="w_raw%d" % g)
-            nc.sync.dma_start(out=wr[:], in_=W[g, :, :].rearrange("(p j) o -> p j o", j=4))
-            w_raw.append(wr)
+            w_raw.append(raw.tile([P, 4, GOUT], BF16, name="w_raw%d" % g))
             for h in range(N_HALF):
-                xr = raw.tile([P, T_IN_HALF, GIN], BF16, name="x_raw%d_%d" % (g, h))
-                nc.sync.dma_start(
-                    out=xr[:],
-                    in_=x[h * HALF : (h + 1) * HALF, g * GIN : (g + 1) * GIN].rearrange("(t p) k -> p t k", p=P),
-                )
-                x_raw.append(xr)
+                x_raw.append(raw.tile([P, T_IN_HALF, GIN], BF16, name="x_raw%d_%d" % (g, h)))
 
-        ident = const.tile([P, P], F32, name="ident")
-        masks.make_identity(nc, ident[:])
+        def load_w(g):
+            nc.sync.dma_start(out=w_raw[g][:], in_=W[g, :, :].rearrange("(p j) o -> p j o", j=4))
 
-        b_rows32 = const.tile([P, P], F32, name="b_rows32")
-        nc.vector.tensor_copy(out=b_rows32[:], in_=b_rows[:])
-        b_ps = ps_x.tile([P, P], F32, name="b_ps", tag="xt")
-        nc.tensor.transpose(out=b_ps[:], in_=b_rows32[:], identity=ident[:])
-        b_col = const.tile([P, G * C_TILES], F32, name="b_col")
-        nc.vector.tensor_copy(out=b_col[:], in_=b_ps[:, 0 : G * C_TILES])
-        pq = const.tile([P, 56], F32, name="pq")
-        nc.vector.tensor_copy(out=pq[:], in_=pq_bf[:])
+        def load_x(j):
+            g, h = divmod(j, N_HALF)
+            nc.sync.dma_start(
+                out=x_raw[j][:],
+                in_=x[h * HALF : (h + 1) * HALF, g * GIN : (g + 1) * GIN].rearrange("(t p) k -> p t k", p=P),
+            )
+
+        load_x(0)
+        load_w(0)
+        load_x(1)
+        for g in range(1, G):
+            load_w(g)
+            load_x(2 * g)
+            load_x(2 * g + 1)
 
         def pcol(g, i):
             return pq[:, 4 * g + i : 4 * g + i + 1]
@@ -87,6 +88,7 @@ def tile_groupkanlayer_kernel(tc, x, W, b, p, q, out_0, out_1):
         xst = {}
         ust = {}
         ost = {}
+        pst = {}
 
         def w_interleave(g, piece):
             if piece == 0:
@@ -121,10 +123,7 @@ def tile_groupkanlayer_kernel(tc, x, W, b, p, q, out_0, out_1):
         def x_copy(j, a):
             dst = xst[j]["grp"][:].bitcast(F32)[:, a * 512 : (a + 1) * 512].rearrange("p (t r u) -> p t r u", t=2, u=2)
             src = xst[j]["xt"][:].rearrange("p t u r -> p t r u")
-            if a == 0:
-                nc.scalar.copy(out=dst, in_=src)
-            else:
-                nc.vector.tensor_copy(out=dst, in_=src)
+            nc.scalar.copy(out=dst, in_=src)
 
         def x_quantize(j):
             xc = stage.tile([P, HALF], U32, name="x_codes", align_bytes=64)
@@ -164,42 +163,40 @@ def tile_groupkanlayer_kernel(tc, x, W, b, p, q, out_0, out_1):
             nc.scalar.activation(out=y_t[:], in_=ust[u]["acc"][:], func=ACT.Identity, bias=bias_of(u), scale=1.0)
             ust[u]["y_t"] = y_t
 
+        def chan(tile3, u):
+            g, j, c = parts(u)
+            return tile3[:, g, c : c + 1]
+
         def g1(u):
             g = parts(u)[0]
-            d_t = work.tile([P, HALF], F32, name="d_t")
-            nc.gpsimd.tensor_scalar(out=d_t[:], in0=ust[u]["y_t"][:], scalar1=qcol(g, 2), scalar2=qcol(g, 1), op0=ALU.mult, op1=ALU.add)
-            ust[u]["d_t"] = d_t
+            h1 = work.tile([P, HALF], F32, name="h1")
+            nc.gpsimd.tensor_scalar(out=h1[:], in0=ust[u]["y_t"][:], scalar1=qcol(g, 2), scalar2=chan(h1b, u), op0=ALU.mult, op1=ALU.add)
+            ust[u]["h1"] = h1
 
         def v1(u):
-            e_t = work.tile([P, HALF], F32, name="e_t")
-            nc.vector.scalar_tensor_tensor(out=e_t[:], in0=ust[u]["acc"][:], scalar=bias_of(u), in1=ust[u]["d_t"][:], op0=ALU.add, op1=ALU.mult)
-            ust[u]["e_t"] = e_t
-
-        def g2(u):
-            g = parts(u)[0]
-            e2_t = work.tile([P, HALF], F32, name="e2_t")
-            nc.gpsimd.tensor_scalar(out=e2_t[:], in0=ust[u]["e_t"][:], scalar1=one_col[:, 0:1], scalar2=qcol(g, 0), op0=ALU.mult, op1=ALU.add)
-            ust[u]["e2_t"] = e2_t
+            h2 = work.tile([P, HALF], F32, name="h2")
+            nc.vector.tensor_tensor(out=h2[:], in0=ust[u]["h1"][:], in1=ust[u]["acc"][:], op=ALU.mult)
+            ust[u]["h2"] = h2
 
         def v2(u):
-            f_t = work.tile([P, HALF], F32, name="f_t")
-            nc.vector.scalar_tensor_tensor(out=f_t[:], in0=ust[u]["acc"][:], scalar=bias_of(u), in1=ust[u]["e2_t"][:], op0=ALU.add, op1=ALU.mult)
-            ust[u]["f_t"] = f_t
+            h3 = work.tile([P, HALF], F32, name="h3")
+            nc.vector.scalar_tensor_tensor(out=h3[:], in0=ust[u]["h2"][:], scalar=chan(f1, u), in1=ust[u]["acc"][:], op0=ALU.add, op1=ALU.mult)
+            ust[u]["h3"] = h3
 
         def s2(u):
             af_t = work.tile([P, HALF], F32, name="af_t")
-            nc.scalar.activation(out=af_t[:], in_=ust[u]["f_t"][:], func=ACT.Abs)
+            nc.scalar.activation(out=af_t[:], in_=ust[u]["h3"][:], func=ACT.Abs, bias=chan(f0, u), scale=1.0)
             ust[u]["af_t"] = af_t
 
         def s3(u):
-            rs_t = work.tile([P, HALF], F32, name="rs_t")
-            nc.scalar.activation(out=rs_t[:], in_=ust[u]["af_t"][:], func=ACT.Abs_reciprocal_sqrt, bias=one_col[:, 0:1], scale=1.0)
-            ust[u]["rs_t"] = rs_t
+            if u % 2 == 0:
+                pst[u // 2] = {"rs": work.tile([P, 2, HALF], F32, name="rs_pair")}
+            nc.scalar.activation(out=pst[u // 2]["rs"][:, u % 2, :], in_=ust[u]["af_t"][:], func=ACT.Abs_reciprocal_sqrt, bias=one_col[:, 0:1], scale=1.0)
 
-        def g3(u):
-            r_t = work.tile([P, HALF], F32, name="r_t")
-            nc.gpsimd.tensor_tensor(out=r_t[:], in0=ust[u]["rs_t"][:], in1=ust[u]["rs_t"][:], op=ALU.mult)
-            ust[u]["r_t"] = r_t
+        def g3(m):
+            r_pair = work.tile([P, 2, HALF], F32, name="r_pair")
+            nc.gpsimd.tensor_tensor(out=r_pair[:], in0=pst[m]["rs"][:], in1=pst[m]["rs"][:], op=ALU.mult)
+            pst[m]["r"] = r_pair
 
         def t_y(u):
             yb = ps_y.tile([P, T_IN_HALF, P], F32, name="yb")
@@ -210,7 +207,7 @@ def tile_groupkanlayer_kernel(tc, x, W, b, p, q, out_0, out_1):
         def t_r(u):
             rb = ps_r.tile([P, T_IN_HALF, P], F32, name="rb")
             for t in range(T_IN_HALF):
-                nc.tensor.transpose(out=rb[:, t, :], in_=ust[u]["r_t"][:, t * P : (t + 1) * P], identity=ident[:])
+                nc.tensor.transpose(out=rb[:, t, :], in_=pst[u // 2]["r"][:, u % 2, t * P : (t + 1) * P], identity=ident[:])
             ust[u]["rb"] = rb
 
         def s4(u):
@@ -259,60 +256,89 @@ def tile_groupkanlayer_kernel(tc, x, W, b, p, q, out_0, out_1):
                 ost[j]["o1"] = outs.tile([P, T_IN_HALF, GOUT], FP8, name="o1")
             nc.scalar.activation(out=ost[j]["o1"][:, t, :], in_=ost[j]["o0"][:, t, :], func=ACT.Copy, scale=Y_SCALE, saturate=False)
 
-        for piece in range(C_TILES):
-            w_interleave(0, piece)
         for a in range(2):
             x_transpose(0, a)
             x_copy(0, a)
+        b_rows32 = const.tile([P, P], F32, name="b_rows32")
+        nc.vector.tensor_copy(out=b_rows32[:], in_=b_rows[:])
+        pq = const.tile([P, 56], F32, name="pq")
+        nc.vector.tensor_copy(out=pq[:], in_=pq_bf[:])
+        wst[0] = {"grp": stage.tile([P, GOUT, 4], BF16, name="w_grp", align_bytes=64)}
+        nc.vector.tensor_copy(out=wst[0]["grp"][:], in_=w_raw[0][:].rearrange("p j o -> p o j"))
         w_quantize(0)
         x_quantize(0)
+        b_ps = ps_x.tile([P, P], F32, name="b_ps", tag="xt")
+        nc.tensor.transpose(out=b_ps[:], in_=b_rows32[:], identity=ident[:])
+        b_col = const.tile([P, G * C_TILES], F32, name="b_col")
+        nc.vector.tensor_copy(out=b_col[:], in_=b_ps[:, 0 : G * C_TILES])
+
+        b3 = b_col[:].rearrange("p (g c) -> p g c", c=C_TILES)
+        qv = pq[:, 32:56].rearrange("p (g k) -> p g k", k=3)
+        q0b = qv[:, :, 0:1].to_broadcast([P, G, C_TILES])
+        q1b = qv[:, :, 1:2].to_broadcast([P, G, C_TILES])
+        q2b = qv[:, :, 2:3].to_broadcast([P, G, C_TILES])
+        t1 = const.tile([P, G, C_TILES], F32, name="t1")
+        nc.vector.tensor_tensor(out=t1[:], in0=b3, in1=q2b, op=ALU.mult)
+        h1b = const.tile([P, G, C_TILES], F32, name="h1b")
+        nc.vector.scalar_tensor_tensor(out=h1b[:], in0=t1[:], scalar=2.0, in1=q1b, op0=ALU.mult, op1=ALU.add)
+        t2 = const.tile([P, G, C_TILES], F32, name="t2")
+        nc.vector.tensor_tensor(out=t2[:], in0=t1[:], in1=q1b, op=ALU.add)
+        t3 = const.tile([P, G, C_TILES], F32, name="t3")
+        nc.vector.tensor_tensor(out=t3[:], in0=t2[:], in1=b3, op=ALU.mult)
+        t4 = const.tile([P, G, C_TILES], F32, name="t4")
+        nc.vector.tensor_tensor(out=t4[:], in0=t3[:], in1=q0b, op=ALU.add)
+        f0 = const.tile([P, G, C_TILES], F32, name="f0")
+        nc.vector.tensor_tensor(out=f0[:], in0=t4[:], in1=b3, op=ALU.mult)
+        t5 = const.tile([P, G, C_TILES], F32, name="t5")
+        nc.vector.tensor_tensor(out=t5[:], in0=h1b[:], in1=b3, op=ALU.mult)
+        f1 = const.tile([P, G, C_TILES], F32, name="f1")
+        nc.vector.tensor_tensor(out=f1[:], in0=t5[:], in1=t4[:], op=ALU.add)
+
 
         V5_LAG = 4
-        for k in range(-1, N_UNITS + V5_LAG + T_IN_HALF + 1):
+        for k in range(-2, N_UNITS + V5_LAG + T_IN_HALF + 1):
+            if ok(k):
+                t_y(k)
+                v1(k)
             if ok(k + 1):
-                mm(k + 1)
+                s1(k + 1)
+            if ok(k + 2):
+                mm(k + 2)
+            if ok(k - 1):
+                s2(k - 1)
+                v3(k - 1)
+            if ok(k + 1):
+                g1(k + 1)
+            if ok(k):
+                s4(k)
+                v2(k)
+            if ok(k - 1):
+                s3(k - 1)
             if ok(k - V5_LAG):
                 v5(k - V5_LAG)
                 if (k - V5_LAG) % C_TILES == C_TILES - 1:
                     jd = (k - V5_LAG) // C_TILES
                     nc.sync.dma_start(out=hbm_view(out_0, jd), in_=ost[jd]["o0"][:])
-            if ok(k - 1):
-                g2(k - 1)
-                s4(k - 1)
-            if ok(k):
-                t_y(k)
-            if ok(k + 1):
-                s1(k + 1)
-            if ok(k - 1):
-                v2(k - 1)
-            if ok(k):
-                g1(k)
-            if ok(k - 1):
-                v3(k - 1)
             kc = k - V5_LAG - C_TILES
             if 0 <= kc < N_UNITS:
                 cast(kc // C_TILES, kc % C_TILES)
                 if kc % C_TILES == C_TILES - 1:
                     nc.sync.dma_start(out=hbm_view(out_1, kc // C_TILES), in_=ost[kc // C_TILES]["o1"][:].bitcast(U8))
+            if (k + 6) % 4 == 0 and 1 <= (k + 6) // 4 < N_IDX:
+                x_transpose((k + 6) // 4, 0)
+                x_copy((k + 6) // 4, 0)
             if (k + 5) % 4 == 0 and 1 <= (k + 5) // 4 < N_IDX:
-                x_transpose((k + 5) // 4, 0)
-                x_copy((k + 5) // 4, 0)
-            if (k + 4) % 4 == 0 and 1 <= (k + 4) // 4 < N_IDX:
-                x_transpose((k + 4) // 4, 1)
-                x_copy((k + 4) // 4, 1)
-            if ok(k):
-                v1(k)
-            if ok(k - 1):
-                s2(k - 1)
-                s3(k - 1)
-            if ok(k - 2):
-                g3(k - 2)
+                x_transpose((k + 5) // 4, 1)
+                x_copy((k + 5) // 4, 1)
             if ok(k - 1):
                 v4(k - 1)
-            if ok(k - 2):
+            if k % 2 == 0 and ok(k - 1):
+                g3((k - 1) // 2)
+            if k % 2 == 1 and ok(k - 2):
+                t_r(k - 3)
                 t_r(k - 2)
-            if (k + 3) % 4 == 0 and 1 <= (k + 3) // 4 < N_IDX:
-                x_quantize((k + 3) // 4)
+            if (k + 4) % 4 == 0 and 1 <= (k + 4) // 4 < N_IDX:
+                x_quantize((k + 4) // 4)
             if k >= 0 and k % 8 < 4 and k // 8 + 1 < G:
                 w_interleave(k // 8 + 1, k % 8)
             if k >= 0 and k % 8 == 4 and k // 8 + 1 < G:

@@ -88,7 +88,6 @@ def tile_groupkanlayer_kernel(tc, x, W, b, p, q, out_0, out_1):
         xst = {}
         ust = {}
         ost = {}
-        pst = {}
 
         def w_interleave(g, piece):
             if piece == 0:
@@ -189,14 +188,14 @@ def tile_groupkanlayer_kernel(tc, x, W, b, p, q, out_0, out_1):
             ust[u]["af_t"] = af_t
 
         def s3(u):
-            if u % 2 == 0:
-                pst[u // 2] = {"rs": work.tile([P, 2, HALF], F32, name="rs_pair")}
-            nc.scalar.activation(out=pst[u // 2]["rs"][:, u % 2, :], in_=ust[u]["af_t"][:], func=ACT.Abs_reciprocal_sqrt, bias=one_col[:, 0:1], scale=1.0)
+            rs_t = work.tile([P, HALF], F32, name="rs_t")
+            nc.scalar.activation(out=rs_t[:], in_=ust[u]["af_t"][:], func=ACT.Abs_reciprocal_sqrt, bias=one_col[:, 0:1], scale=1.0)
+            ust[u]["rs_t"] = rs_t
 
-        def g3(m):
-            r_pair = work.tile([P, 2, HALF], F32, name="r_pair")
-            nc.gpsimd.tensor_tensor(out=r_pair[:], in0=pst[m]["rs"][:], in1=pst[m]["rs"][:], op=ALU.mult)
-            pst[m]["r"] = r_pair
+        def g3(u):
+            r_t = work.tile([P, HALF], F32, name="r_t")
+            nc.gpsimd.tensor_tensor(out=r_t[:], in0=ust[u]["rs_t"][:], in1=ust[u]["rs_t"][:], op=ALU.mult)
+            ust[u]["r_t"] = r_t
 
         def t_y(u):
             yb = ps_y.tile([P, T_IN_HALF, P], F32, name="yb")
@@ -207,7 +206,7 @@ def tile_groupkanlayer_kernel(tc, x, W, b, p, q, out_0, out_1):
         def t_r(u):
             rb = ps_r.tile([P, T_IN_HALF, P], F32, name="rb")
             for t in range(T_IN_HALF):
-                nc.tensor.transpose(out=rb[:, t, :], in_=pst[u // 2]["r"][:, u % 2, t * P : (t + 1) * P], identity=ident[:])
+                nc.tensor.transpose(out=rb[:, t, :], in_=ust[u]["r_t"][:, t * P : (t + 1) * P], identity=ident[:])
             ust[u]["rb"] = rb
 
         def s4(u):
@@ -223,7 +222,7 @@ def tile_groupkanlayer_kernel(tc, x, W, b, p, q, out_0, out_1):
 
         def v4(u):
             g = parts(u)[0]
-            c_d = work.tile([P, T_IN_HALF, P], F32, name="c_d")
+            c_d = work.tile([P, T_IN_HALF, P], F32, name="c_d", bufs=5)
             nc.vector.scalar_tensor_tensor(
                 out=c_d[:].rearrange("p t n -> p (t n)"),
                 in0=ust[u]["b_d"][:],
@@ -295,8 +294,10 @@ def tile_groupkanlayer_kernel(tc, x, W, b, p, q, out_0, out_1):
         nc.vector.tensor_tensor(out=f1[:], in0=t5[:], in1=t4[:], op=ALU.add)
 
 
-        V5_LAG = 4
-        for k in range(-2, N_UNITS + V5_LAG + T_IN_HALF + 1):
+        V5_LAG = 5
+        for k in range(-3, N_UNITS + V5_LAG + C_TILES + 1):
+            if (k + 4) % 4 == 0 and 1 <= (k + 4) // 4 < N_IDX:
+                x_quantize((k + 4) // 4)
             if ok(k):
                 t_y(k)
                 v1(k)
@@ -306,40 +307,41 @@ def tile_groupkanlayer_kernel(tc, x, W, b, p, q, out_0, out_1):
                 mm(k + 2)
             if ok(k - 1):
                 s2(k - 1)
-                v3(k - 1)
-            if ok(k + 1):
-                g1(k + 1)
-            if ok(k):
-                s4(k)
-                v2(k)
-            if ok(k - 1):
-                s3(k - 1)
             if ok(k - V5_LAG):
                 v5(k - V5_LAG)
                 if (k - V5_LAG) % C_TILES == C_TILES - 1:
                     jd = (k - V5_LAG) // C_TILES
                     nc.sync.dma_start(out=hbm_view(out_0, jd), in_=ost[jd]["o0"][:])
+            if (k + 6) % 4 == 0 and 1 <= (k + 6) // 4 < N_IDX:
+                x_copy((k + 6) // 4, 0)
+            if (k + 5) % 4 == 0 and 1 <= (k + 5) // 4 < N_IDX:
+                x_copy((k + 5) // 4, 1)
+            if ok(k + 1):
+                g1(k + 1)
             kc = k - V5_LAG - C_TILES
             if 0 <= kc < N_UNITS:
                 cast(kc // C_TILES, kc % C_TILES)
                 if kc % C_TILES == C_TILES - 1:
                     nc.sync.dma_start(out=hbm_view(out_1, kc // C_TILES), in_=ost[kc // C_TILES]["o1"][:].bitcast(U8))
-            if (k + 6) % 4 == 0 and 1 <= (k + 6) // 4 < N_IDX:
-                x_transpose((k + 6) // 4, 0)
-                x_copy((k + 6) // 4, 0)
-            if (k + 5) % 4 == 0 and 1 <= (k + 5) // 4 < N_IDX:
-                x_transpose((k + 5) // 4, 1)
-                x_copy((k + 5) // 4, 1)
             if ok(k - 1):
-                v4(k - 1)
-            if k % 2 == 0 and ok(k - 1):
-                g3((k - 1) // 2)
-            if k % 2 == 1 and ok(k - 2):
-                t_r(k - 3)
-                t_r(k - 2)
-            if (k + 4) % 4 == 0 and 1 <= (k + 4) // 4 < N_IDX:
-                x_quantize((k + 4) // 4)
+                s3(k - 1)
             if k >= 0 and k % 8 < 4 and k // 8 + 1 < G:
                 w_interleave(k // 8 + 1, k % 8)
+            if ok(k - 1):
+                v3(k - 1)
+            if ok(k):
+                v2(k)
+            if (k + 7) % 4 == 0 and 1 <= (k + 7) // 4 < N_IDX:
+                x_transpose((k + 7) // 4, 0)
+            if (k + 6) % 4 == 0 and 1 <= (k + 6) // 4 < N_IDX:
+                x_transpose((k + 6) // 4, 1)
+            if ok(k):
+                s4(k)
+            if ok(k - 1):
+                v4(k - 1)
+            if ok(k - 2):
+                g3(k - 2)
+            if ok(k - 3):
+                t_r(k - 3)
             if k >= 0 and k % 8 == 4 and k // 8 + 1 < G:
                 w_quantize(k // 8 + 1)

@@ -70,7 +70,11 @@ def tile_groupkanlayer_kernel(tc, x, W, b, p, q, out_0, out_1):
                 in_=x[h * HALF : (h + 1) * HALF, g * GIN : (g + 1) * GIN].rearrange("(t p) k -> p t k", p=P),
             )
 
-        load_x(0)
+        for a in range(2):
+            nc.sync.dma_start(
+                out=x_raw[0][:, 2 * a : 2 * a + 2, :],
+                in_=x[2 * a * P : (2 * a + 2) * P, 0:GIN].rearrange("(t p) k -> p t k", p=P),
+            )
         load_w(0)
         load_x(1)
         for g in range(1, G):
@@ -109,19 +113,22 @@ def tile_groupkanlayer_kernel(tc, x, W, b, p, q, out_0, out_1):
             wst[g]["codes"] = wc
             wst[g]["scales"] = ws
 
-        def x_transpose(j, a):
+        def x_transpose(j, a, borrow=False):
             if a == 0:
                 xst[j] = {"grp": stage.tile([P, HALF * 4], BF16, name="x_grp", align_bytes=64)}
             xw = x_raw[j][:].bitcast(F32)
-            xt = ps_x.tile([P, 2, 2, P], F32, name="xt", tag="xt")
+            if borrow:
+                xt = ps_r.tile([P, 2, 2, P], F32, name="xt_borrowed", tag="rb")
+            else:
+                xt = ps_x.tile([P, 2, 2, P], F32, name="xt", tag="xt")
             for tt in range(2):
                 for u in range(2):
                     nc.tensor.transpose(out=xt[:, tt, u, :], in_=xw[:, 2 * a + tt, u : GIN // 2 : 2], identity=ident[:])
-            xst[j]["xt"] = xt
+            xst[j]["xt%d" % a] = xt
 
         def x_copy(j, a):
             dst = xst[j]["grp"][:].bitcast(F32)[:, a * 512 : (a + 1) * 512].rearrange("p (t r u) -> p t r u", t=2, u=2)
-            src = xst[j]["xt"][:].rearrange("p t u r -> p t r u")
+            src = xst[j]["xt%d" % a][:].rearrange("p t u r -> p t r u")
             nc.scalar.copy(out=dst, in_=src)
 
         def x_quantize(j):
@@ -204,7 +211,7 @@ def tile_groupkanlayer_kernel(tc, x, W, b, p, q, out_0, out_1):
             ust[u]["yb"] = yb
 
         def t_r(u):
-            rb = ps_r.tile([P, T_IN_HALF, P], F32, name="rb")
+            rb = ps_r.tile([P, T_IN_HALF, P], F32, name="rb", tag="rb")
             for t in range(T_IN_HALF):
                 nc.tensor.transpose(out=rb[:, t, :], in_=ust[u]["r_t"][:, t * P : (t + 1) * P], identity=ident[:])
             ust[u]["rb"] = rb
@@ -255,21 +262,22 @@ def tile_groupkanlayer_kernel(tc, x, W, b, p, q, out_0, out_1):
                 ost[j]["o1"] = outs.tile([P, T_IN_HALF, GOUT], FP8, name="o1")
             nc.scalar.activation(out=ost[j]["o1"][:, t, :], in_=ost[j]["o0"][:, t, :], func=ACT.Copy, scale=Y_SCALE, saturate=False)
 
-        for a in range(2):
-            x_transpose(0, a)
-            x_copy(0, a)
-        b_rows32 = const.tile([P, P], F32, name="b_rows32")
-        nc.vector.tensor_copy(out=b_rows32[:], in_=b_rows[:])
-        pq = const.tile([P, 56], F32, name="pq")
-        nc.vector.tensor_copy(out=pq[:], in_=pq_bf[:])
+        x_transpose(0, 0)
+        x_transpose(0, 1, borrow=True)
+        x_copy(0, 0)
+        x_copy(0, 1)
         wst[0] = {"grp": stage.tile([P, GOUT, 4], BF16, name="w_grp", align_bytes=64)}
         nc.vector.tensor_copy(out=wst[0]["grp"][:], in_=w_raw[0][:].rearrange("p j o -> p o j"))
-        w_quantize(0)
         x_quantize(0)
+        w_quantize(0)
+        b_rows32 = const.tile([P, P], F32, name="b_rows32")
+        nc.scalar.copy(out=b_rows32[:], in_=b_rows[:])
         b_ps = ps_x.tile([P, P], F32, name="b_ps", tag="xt")
         nc.tensor.transpose(out=b_ps[:], in_=b_rows32[:], identity=ident[:])
         b_col = const.tile([P, G * C_TILES], F32, name="b_col")
-        nc.vector.tensor_copy(out=b_col[:], in_=b_ps[:, 0 : G * C_TILES])
+        nc.scalar.copy(out=b_col[:], in_=b_ps[:, 0 : G * C_TILES])
+        pq = const.tile([P, 56], F32, name="pq")
+        nc.scalar.copy(out=pq[:], in_=pq_bf[:])
 
         b3 = b_col[:].rearrange("p (g c) -> p g c", c=C_TILES)
         qv = pq[:, 32:56].rearrange("p (g k) -> p g k", k=3)
@@ -298,6 +306,8 @@ def tile_groupkanlayer_kernel(tc, x, W, b, p, q, out_0, out_1):
         for k in range(-3, N_UNITS + V5_LAG + C_TILES + 1):
             if (k + 4) % 4 == 0 and 1 <= (k + 4) // 4 < N_IDX:
                 x_quantize((k + 4) // 4)
+            if k >= 0 and k % 8 == 5 and k // 8 + 1 < G:
+                w_quantize(k // 8 + 1)
             if ok(k):
                 t_y(k)
                 v1(k)
@@ -343,5 +353,3 @@ def tile_groupkanlayer_kernel(tc, x, W, b, p, q, out_0, out_1):
                 g3(k - 2)
             if ok(k - 3):
                 t_r(k - 3)
-            if k >= 0 and k % 8 == 4 and k // 8 + 1 < G:
-                w_quantize(k // 8 + 1)

@@ -35,7 +35,7 @@ def tile_groupkanlayer_kernel(tc, x, W, b, p, q, out_0, out_1):
         outs = ctx.enter_context(tc.tile_pool(name="outs", bufs=3))
         ps_x = ctx.enter_context(tc.psum_pool(name="ps_x", bufs=1))
         ps_acc = ctx.enter_context(tc.psum_pool(name="ps_acc", bufs=3))
-        ps_y = ctx.enter_context(tc.psum_pool(name="ps_y", bufs=2))
+        ps_n = ctx.enter_context(tc.psum_pool(name="ps_n", bufs=2))
         ps_r = ctx.enter_context(tc.psum_pool(name="ps_r", bufs=2))
         ctx.enter_context(tc.manual_schedule())
 
@@ -129,7 +129,10 @@ def tile_groupkanlayer_kernel(tc, x, W, b, p, q, out_0, out_1):
         def x_copy(j, a):
             dst = xst[j]["grp"][:].bitcast(F32)[:, a * 512 : (a + 1) * 512].rearrange("p (t r u) -> p t r u", t=2, u=2)
             src = xst[j]["xt%d" % a][:].rearrange("p t u r -> p t r u")
-            nc.scalar.copy(out=dst, in_=src)
+            if a == 1 and j % 2 == 1:
+                nc.vector.tensor_copy(out=dst, in_=src)
+            else:
+                nc.scalar.copy(out=dst, in_=src)
 
         def x_quantize(j):
             xc = stage.tile([P, HALF], U32, name="x_codes", align_bytes=64)
@@ -173,11 +176,26 @@ def tile_groupkanlayer_kernel(tc, x, W, b, p, q, out_0, out_1):
             g, j, c = parts(u)
             return tile3[:, g, c : c + 1]
 
+        def on_pool(u):
+            return u % 8 in (5, 7)
+
         def g1(u):
             g = parts(u)[0]
             h1 = work.tile([P, HALF], F32, name="h1")
             nc.gpsimd.tensor_scalar(out=h1[:], in0=ust[u]["y_t"][:], scalar1=qcol(g, 2), scalar2=chan(h1b, u), op0=ALU.mult, op1=ALU.add)
             ust[u]["h1"] = h1
+
+        def g2(u):
+            g = parts(u)[0]
+            a_c = work.tile([P, HALF], F32, name="a_c")
+            nc.gpsimd.tensor_scalar(
+                out=a_c[:], in0=ust[u]["y_t"][:], scalar1=pcol(g, 3), scalar2=chan(u2 if on_pool(u) else ab, u), op0=ALU.mult, op1=ALU.add
+            )
+            ust[u]["a_c"] = a_c
+            if on_pool(u):
+                bb = work.tile([P, HALF], F32, name="bb")
+                nc.gpsimd.tensor_tensor(out=bb[:], in0=a_c[:], in1=ust[u]["y_t"][:], op=ALU.mult)
+                ust[u]["bb"] = bb
 
         def v1(u):
             h2 = work.tile([P, HALF], F32, name="h2")
@@ -189,6 +207,20 @@ def tile_groupkanlayer_kernel(tc, x, W, b, p, q, out_0, out_1):
             nc.vector.scalar_tensor_tensor(out=h3[:], in0=ust[u]["h2"][:], scalar=chan(f1, u), in1=ust[u]["acc"][:], op0=ALU.add, op1=ALU.mult)
             ust[u]["h3"] = h3
 
+        def v3(u):
+            if on_pool(u):
+                return
+            bb = work.tile([P, HALF], F32, name="bb")
+            nc.vector.tensor_tensor(out=bb[:], in0=ust[u]["a_c"][:], in1=ust[u]["acc"][:], op=ALU.mult)
+            ust[u]["bb"] = bb
+
+        def v4(u):
+            c_t = work.tile([P, HALF], F32, name="c_t", bufs=5)
+            nc.vector.scalar_tensor_tensor(
+                out=c_t[:], in0=ust[u]["bb"][:], scalar=chan(u4 if on_pool(u) else e1, u), in1=ust[u]["acc"][:], op0=ALU.add, op1=ALU.mult
+            )
+            ust[u]["c_t"] = c_t
+
         def s2(u):
             af_t = work.tile([P, HALF], F32, name="af_t")
             nc.scalar.activation(out=af_t[:], in_=ust[u]["h3"][:], func=ACT.Abs, bias=chan(f0, u), scale=1.0)
@@ -199,59 +231,29 @@ def tile_groupkanlayer_kernel(tc, x, W, b, p, q, out_0, out_1):
             nc.scalar.activation(out=rs_t[:], in_=ust[u]["af_t"][:], func=ACT.Abs_reciprocal_sqrt, bias=one_col[:, 0:1], scale=1.0)
             ust[u]["rs_t"] = rs_t
 
-        def g3(u):
-            r_t = work.tile([P, HALF], F32, name="r_t")
-            nc.gpsimd.tensor_tensor(out=r_t[:], in0=ust[u]["rs_t"][:], in1=ust[u]["rs_t"][:], op=ALU.mult)
-            ust[u]["r_t"] = r_t
-
-        def t_y(u):
-            yb = ps_y.tile([P, T_IN_HALF, P], F32, name="yb")
-            for t in range(T_IN_HALF):
-                nc.tensor.transpose(out=yb[:, t, :], in_=ust[u]["y_t"][:, t * P : (t + 1) * P], identity=ident[:])
-            ust[u]["yb"] = yb
-
         def t_r(u):
             rb = ps_r.tile([P, T_IN_HALF, P], F32, name="rb", tag="rb")
             for t in range(T_IN_HALF):
-                nc.tensor.transpose(out=rb[:, t, :], in_=ust[u]["r_t"][:, t * P : (t + 1) * P], identity=ident[:])
+                nc.tensor.transpose(out=rb[:, t, :], in_=ust[u]["rs_t"][:, t * P : (t + 1) * P], identity=ident[:])
             ust[u]["rb"] = rb
 
+        def t_n(u):
+            nb = ps_n.tile([P, T_IN_HALF, P], F32, name="nb")
+            for t in range(T_IN_HALF):
+                nc.tensor.matmul(out=nb[:, t, :], lhsT=chan(e0, u).to_broadcast([P, P]), rhs=ident[:], is_transpose=True, start=True, stop=False)
+                nc.tensor.matmul(out=nb[:, t, :], lhsT=ust[u]["c_t"][:, t * P : (t + 1) * P], rhs=ident[:], is_transpose=True, start=False, stop=True)
+            ust[u]["nb"] = nb
+
         def s4(u):
-            g = parts(u)[0]
-            a_d = work.tile([P, HALF], F32, name="a_d")
-            nc.scalar.activation(out=a_d[:], in_=ust[u]["yb"][:].rearrange("p t n -> p (t n)"), func=ACT.Identity, bias=pcol(g, 2), scale=pcol(g, 3))
-            ust[u]["a_d"] = a_d
-
-        def v3(u):
-            b_d = work.tile([P, HALF], F32, name="b_d")
-            nc.vector.tensor_tensor(out=b_d[:], in0=ust[u]["a_d"][:], in1=ust[u]["yb"][:].rearrange("p t n -> p (t n)"), op=ALU.mult)
-            ust[u]["b_d"] = b_d
-
-        def v4(u):
-            g = parts(u)[0]
-            c_d = work.tile([P, T_IN_HALF, P], F32, name="c_d", bufs=5)
-            nc.vector.scalar_tensor_tensor(
-                out=c_d[:].rearrange("p t n -> p (t n)"),
-                in0=ust[u]["b_d"][:],
-                scalar=pcol(g, 1),
-                in1=ust[u]["yb"][:].rearrange("p t n -> p (t n)"),
-                op0=ALU.add,
-                op1=ALU.mult,
-            )
-            ust[u]["c_d"] = c_d
+            r_d = work.tile([P, T_IN_HALF, P], F32, name="r_d")
+            nc.scalar.activation(out=r_d[:].rearrange("p t n -> p (t n)"), in_=ust[u]["rb"][:].rearrange("p t n -> p (t n)"), func=ACT.Square)
+            ust[u]["r_d"] = r_d
 
         def v5(u):
             g, j, c = parts(u)
             if c == 0:
                 ost[j] = {"o0": outs.tile([P, T_IN_HALF, GOUT], F32, name="o0")}
-            nc.vector.scalar_tensor_tensor(
-                out=ost[j]["o0"][:, :, c * P : (c + 1) * P],
-                in0=ust[u]["c_d"][:],
-                scalar=pcol(g, 0),
-                in1=ust[u]["rb"][:],
-                op0=ALU.add,
-                op1=ALU.mult,
-            )
+            nc.vector.tensor_tensor(out=ost[j]["o0"][:, :, c * P : (c + 1) * P], in0=ust[u]["r_d"][:], in1=ust[u]["nb"][:], op=ALU.mult)
 
         def hbm_view(dram, j):
             g, h = divmod(j, N_HALF)
@@ -260,7 +262,10 @@ def tile_groupkanlayer_kernel(tc, x, W, b, p, q, out_0, out_1):
         def cast(j, t):
             if t == 0:
                 ost[j]["o1"] = outs.tile([P, T_IN_HALF, GOUT], FP8, name="o1")
-            nc.scalar.activation(out=ost[j]["o1"][:, t, :], in_=ost[j]["o0"][:, t, :], func=ACT.Copy, scale=Y_SCALE, saturate=False)
+            if j >= 14:
+                nc.vector.tensor_scalar(out=ost[j]["o1"][:, t, :], in0=ost[j]["o0"][:, t, :], scalar1=Y_SCALE, scalar2=None, op0=ALU.mult, saturate=False)
+            else:
+                nc.scalar.activation(out=ost[j]["o1"][:, t, :], in_=ost[j]["o0"][:, t, :], func=ACT.Copy, scale=Y_SCALE, saturate=False)
 
         x_transpose(0, 0)
         x_transpose(0, 1, borrow=True)
@@ -284,72 +289,87 @@ def tile_groupkanlayer_kernel(tc, x, W, b, p, q, out_0, out_1):
         q0b = qv[:, :, 0:1].to_broadcast([P, G, C_TILES])
         q1b = qv[:, :, 1:2].to_broadcast([P, G, C_TILES])
         q2b = qv[:, :, 2:3].to_broadcast([P, G, C_TILES])
-        t1 = const.tile([P, G, C_TILES], F32, name="t1")
-        nc.vector.tensor_tensor(out=t1[:], in0=b3, in1=q2b, op=ALU.mult)
-        h1b = const.tile([P, G, C_TILES], F32, name="h1b")
+        pv = pq[:, 0:32].rearrange("p (g k) -> p g k", k=4)
+        p0b = pv[:, :, 0:1].to_broadcast([P, G, C_TILES])
+        p1b = pv[:, :, 1:2].to_broadcast([P, G, C_TILES])
+        p2b = pv[:, :, 2:3].to_broadcast([P, G, C_TILES])
+        p3b = pv[:, :, 3:4].to_broadcast([P, G, C_TILES])
+
+        def ctile(name):
+            return const.tile([P, G, C_TILES], F32, name=name)
+
+        def tt(out, in0, in1, op):
+            nc.vector.tensor_tensor(out=out[:], in0=in0, in1=in1, op=op)
+
+        t1, u1, h1b, ab, t2, u2, t3, u3 = ctile("t1"), ctile("u1"), ctile("h1b"), ctile("ab"), ctile("t2"), ctile("u2"), ctile("t3"), ctile("u3")
+        t4, u4, f0, u6, t5, u5, f1, e1, e0 = ctile("t4"), ctile("u4"), ctile("f0"), ctile("u6"), ctile("t5"), ctile("u5"), ctile("f1"), ctile("e1"), ctile("e0")
+        tt(t1, b3, q2b, ALU.mult)
+        tt(u1, b3, p3b, ALU.mult)
         nc.vector.scalar_tensor_tensor(out=h1b[:], in0=t1[:], scalar=2.0, in1=q1b, op0=ALU.mult, op1=ALU.add)
-        t2 = const.tile([P, G, C_TILES], F32, name="t2")
-        nc.vector.tensor_tensor(out=t2[:], in0=t1[:], in1=q1b, op=ALU.add)
-        t3 = const.tile([P, G, C_TILES], F32, name="t3")
-        nc.vector.tensor_tensor(out=t3[:], in0=t2[:], in1=b3, op=ALU.mult)
-        t4 = const.tile([P, G, C_TILES], F32, name="t4")
-        nc.vector.tensor_tensor(out=t4[:], in0=t3[:], in1=q0b, op=ALU.add)
-        f0 = const.tile([P, G, C_TILES], F32, name="f0")
-        nc.vector.tensor_tensor(out=f0[:], in0=t4[:], in1=b3, op=ALU.mult)
-        t5 = const.tile([P, G, C_TILES], F32, name="t5")
-        nc.vector.tensor_tensor(out=t5[:], in0=h1b[:], in1=b3, op=ALU.mult)
-        f1 = const.tile([P, G, C_TILES], F32, name="f1")
-        nc.vector.tensor_tensor(out=f1[:], in0=t5[:], in1=t4[:], op=ALU.add)
+        nc.vector.scalar_tensor_tensor(out=ab[:], in0=u1[:], scalar=2.0, in1=p2b, op0=ALU.mult, op1=ALU.add)
+        tt(t2, t1[:], q1b, ALU.add)
+        tt(u2, u1[:], p2b, ALU.add)
+        tt(t3, t2[:], b3, ALU.mult)
+        tt(u3, u2[:], b3, ALU.mult)
+        tt(t4, t3[:], q0b, ALU.add)
+        tt(u4, u3[:], p1b, ALU.add)
+        tt(f0, t4[:], b3, ALU.mult)
+        tt(u6, u4[:], b3, ALU.mult)
+        tt(t5, h1b[:], b3, ALU.mult)
+        tt(u5, ab[:], b3, ALU.mult)
+        tt(f1, t5[:], t4[:], ALU.add)
+        tt(e1, u5[:], u4[:], ALU.add)
+        tt(e0, u6[:], p0b, ALU.add)
 
-
-        V5_LAG = 5
+        V5_LAG = 4
         for k in range(-3, N_UNITS + V5_LAG + C_TILES + 1):
             if (k + 4) % 4 == 0 and 1 <= (k + 4) // 4 < N_IDX:
                 x_quantize((k + 4) // 4)
             if k >= 0 and k % 8 == 5 and k // 8 + 1 < G:
                 w_quantize(k // 8 + 1)
-            if ok(k):
-                t_y(k)
-                v1(k)
             if ok(k + 1):
                 s1(k + 1)
             if ok(k + 2):
                 mm(k + 2)
+            if ok(k):
+                v1(k)
+            if ok(k + 1):
+                g1(k + 1)
+            if ok(k + 1):
+                g2(k + 1)
             if ok(k - 1):
                 s2(k - 1)
-            if ok(k - V5_LAG):
-                v5(k - V5_LAG)
-                if (k - V5_LAG) % C_TILES == C_TILES - 1:
-                    jd = (k - V5_LAG) // C_TILES
-                    nc.sync.dma_start(out=hbm_view(out_0, jd), in_=ost[jd]["o0"][:])
+            if ok(k):
+                v3(k)
+            if ok(k - 2):
+                t_r(k - 2)
             if (k + 6) % 4 == 0 and 1 <= (k + 6) // 4 < N_IDX:
                 x_copy((k + 6) // 4, 0)
             if (k + 5) % 4 == 0 and 1 <= (k + 5) // 4 < N_IDX:
                 x_copy((k + 5) // 4, 1)
-            if ok(k + 1):
-                g1(k + 1)
             kc = k - V5_LAG - C_TILES
             if 0 <= kc < N_UNITS:
                 cast(kc // C_TILES, kc % C_TILES)
                 if kc % C_TILES == C_TILES - 1:
                     nc.sync.dma_start(out=hbm_view(out_1, kc // C_TILES), in_=ost[kc // C_TILES]["o1"][:].bitcast(U8))
+            if ok(k):
+                v2(k)
             if ok(k - 1):
                 s3(k - 1)
             if k >= 0 and k % 8 < 4 and k // 8 + 1 < G:
                 w_interleave(k // 8 + 1, k % 8)
-            if ok(k - 1):
-                v3(k - 1)
+            if ok(k - 3):
+                t_n(k - 3)
             if ok(k):
-                v2(k)
+                v4(k)
+            if ok(k - 3):
+                s4(k - 3)
             if (k + 7) % 4 == 0 and 1 <= (k + 7) // 4 < N_IDX:
                 x_transpose((k + 7) // 4, 0)
             if (k + 6) % 4 == 0 and 1 <= (k + 6) // 4 < N_IDX:
                 x_transpose((k + 6) // 4, 1)
-            if ok(k):
-                s4(k)
-            if ok(k - 1):
-                v4(k - 1)
-            if ok(k - 2):
-                g3(k - 2)
-            if ok(k - 3):
-                t_r(k - 3)
+            if ok(k - V5_LAG):
+                v5(k - V5_LAG)
+                if (k - V5_LAG) % C_TILES == C_TILES - 1:
+                    jd = (k - V5_LAG) // C_TILES
+                    nc.sync.dma_start(out=hbm_view(out_0, jd), in_=ost[jd]["o0"][:])

@@ -148,14 +148,10 @@ def tile_groupkanlayer_kernel(tc, x, W, b, p, q, out_0, out_1):
             j, c = divmod(u, C_TILES)
             return j // N_HALF, j, c
 
-        def bias_of(u):
-            g, j, c = parts(u)
-            return b_col[:, g * C_TILES + c : g * C_TILES + c + 1]
-
         def mm(u):
             g, j, c = parts(u)
             cs = slice(c * P, (c + 1) * P)
-            acc = ps_acc.tile([P, HALF], F32, name="acc")
+            acc = ps_acc.tile([P, HALF], F32, name="acc", tag="acc")
             nc.tensor.matmul_mx(
                 out=acc[:],
                 lhsT=wst[g]["codes"][:, cs].bitcast(FP8X4),
@@ -168,9 +164,9 @@ def tile_groupkanlayer_kernel(tc, x, W, b, p, q, out_0, out_1):
             ust[u] = {"acc": acc}
 
         def s1(u):
-            y_t = work.tile([P, HALF], F32, name="y_t")
-            nc.scalar.activation(out=y_t[:], in_=ust[u]["acc"][:], func=ACT.Identity, bias=bias_of(u), scale=1.0)
-            ust[u]["y_t"] = y_t
+            s_t = work.tile([P, HALF], F32, name="s_t")
+            nc.scalar.copy(out=s_t[:], in_=ust[u]["acc"][:])
+            ust[u]["s_t"] = s_t
 
         def chan(tile3, u):
             g, j, c = parts(u)
@@ -182,19 +178,17 @@ def tile_groupkanlayer_kernel(tc, x, W, b, p, q, out_0, out_1):
         def g1(u):
             g = parts(u)[0]
             h1 = work.tile([P, HALF], F32, name="h1")
-            nc.gpsimd.tensor_scalar(out=h1[:], in0=ust[u]["y_t"][:], scalar1=qcol(g, 2), scalar2=chan(h1b, u), op0=ALU.mult, op1=ALU.add)
+            nc.gpsimd.tensor_scalar(out=h1[:], in0=ust[u]["s_t"][:], scalar1=qcol(g, 2), scalar2=chan(f2, u), op0=ALU.mult, op1=ALU.add)
             ust[u]["h1"] = h1
 
         def g2(u):
             g = parts(u)[0]
             a_c = work.tile([P, HALF], F32, name="a_c")
-            nc.gpsimd.tensor_scalar(
-                out=a_c[:], in0=ust[u]["y_t"][:], scalar1=pcol(g, 3), scalar2=chan(u2 if on_pool(u) else ab, u), op0=ALU.mult, op1=ALU.add
-            )
+            nc.gpsimd.tensor_scalar(out=a_c[:], in0=ust[u]["s_t"][:], scalar1=pcol(g, 3), scalar2=chan(e2, u), op0=ALU.mult, op1=ALU.add)
             ust[u]["a_c"] = a_c
             if on_pool(u):
                 bb = work.tile([P, HALF], F32, name="bb")
-                nc.gpsimd.tensor_tensor(out=bb[:], in0=a_c[:], in1=ust[u]["y_t"][:], op=ALU.mult)
+                nc.gpsimd.tensor_tensor(out=bb[:], in0=a_c[:], in1=ust[u]["s_t"][:], op=ALU.mult)
                 ust[u]["bb"] = bb
 
         def v1(u):
@@ -216,9 +210,7 @@ def tile_groupkanlayer_kernel(tc, x, W, b, p, q, out_0, out_1):
 
         def v4(u):
             c_t = work.tile([P, HALF], F32, name="c_t", bufs=5)
-            nc.vector.scalar_tensor_tensor(
-                out=c_t[:], in0=ust[u]["bb"][:], scalar=chan(u4 if on_pool(u) else e1, u), in1=ust[u]["acc"][:], op0=ALU.add, op1=ALU.mult
-            )
+            nc.vector.scalar_tensor_tensor(out=c_t[:], in0=ust[u]["bb"][:], scalar=chan(e1, u), in1=ust[u]["acc"][:], op0=ALU.add, op1=ALU.mult)
             ust[u]["c_t"] = c_t
 
         def s2(u):
@@ -238,7 +230,10 @@ def tile_groupkanlayer_kernel(tc, x, W, b, p, q, out_0, out_1):
             ust[u]["rb"] = rb
 
         def t_n(u):
-            nb = ps_n.tile([P, T_IN_HALF, P], F32, name="nb")
+            if u >= 61:
+                nb = ps_acc.tile([P, T_IN_HALF, P], F32, name="nb_borrowed", tag="acc")
+            else:
+                nb = ps_n.tile([P, T_IN_HALF, P], F32, name="nb")
             for t in range(T_IN_HALF):
                 nc.tensor.matmul(out=nb[:, t, :], lhsT=chan(e0, u).to_broadcast([P, P]), rhs=ident[:], is_transpose=True, start=True, stop=False)
                 nc.tensor.matmul(out=nb[:, t, :], lhsT=ust[u]["c_t"][:, t * P : (t + 1) * P], rhs=ident[:], is_transpose=True, start=False, stop=True)
@@ -249,8 +244,23 @@ def tile_groupkanlayer_kernel(tc, x, W, b, p, q, out_0, out_1):
             nc.scalar.activation(out=r_d[:].rearrange("p t n -> p (t n)"), in_=ust[u]["rb"][:].rearrange("p t n -> p (t n)"), func=ACT.Square)
             ust[u]["r_d"] = r_d
 
+        def hbm_unit_view(dram, u):
+            g, j, c = parts(u)
+            h = j % N_HALF
+            return dram[h * HALF : (h + 1) * HALF, g * GOUT + c * P : g * GOUT + (c + 1) * P].rearrange("(t p) n -> p t n", p=P)
+
         def v5(u):
             g, j, c = parts(u)
+            if j == N_IDX - 1:
+                o0u = outs.tile([P, T_IN_HALF, P], F32, name="o0u", bufs=4)
+                nc.vector.tensor_tensor(out=o0u[:], in0=ust[u]["r_d"][:], in1=ust[u]["nb"][:], op=ALU.mult)
+                nc.sync.dma_start(out=hbm_unit_view(out_0, u), in_=o0u[:])
+                o1u = outs.tile([P, T_IN_HALF, P], FP8, name="o1u", bufs=4)
+                nc.vector.tensor_scalar(
+                    out=o1u[:].rearrange("p t n -> p (t n)"), in0=o0u[:].rearrange("p t n -> p (t n)"), scalar1=Y_SCALE, scalar2=None, op0=ALU.mult, saturate=False
+                )
+                nc.sync.dma_start(out=hbm_unit_view(out_1, u), in_=o1u[:].bitcast(U8))
+                return
             if c == 0:
                 ost[j] = {"o0": outs.tile([P, T_IN_HALF, GOUT], F32, name="o0")}
             nc.vector.tensor_tensor(out=ost[j]["o0"][:, :, c * P : (c + 1) * P], in0=ust[u]["r_d"][:], in1=ust[u]["nb"][:], op=ALU.mult)
@@ -302,6 +312,7 @@ def tile_groupkanlayer_kernel(tc, x, W, b, p, q, out_0, out_1):
             nc.vector.tensor_tensor(out=out[:], in0=in0, in1=in1, op=op)
 
         t1, u1, h1b, ab, t2, u2, t3, u3 = ctile("t1"), ctile("u1"), ctile("h1b"), ctile("ab"), ctile("t2"), ctile("u2"), ctile("t3"), ctile("u3")
+        f2, e2 = ctile("f2"), ctile("e2")
         t4, u4, f0, u6, t5, u5, f1, e1, e0 = ctile("t4"), ctile("u4"), ctile("f0"), ctile("u6"), ctile("t5"), ctile("u5"), ctile("f1"), ctile("e1"), ctile("e0")
         tt(t1, b3, q2b, ALU.mult)
         tt(u1, b3, p3b, ALU.mult)
@@ -309,6 +320,8 @@ def tile_groupkanlayer_kernel(tc, x, W, b, p, q, out_0, out_1):
         nc.vector.scalar_tensor_tensor(out=ab[:], in0=u1[:], scalar=2.0, in1=p2b, op0=ALU.mult, op1=ALU.add)
         tt(t2, t1[:], q1b, ALU.add)
         tt(u2, u1[:], p2b, ALU.add)
+        tt(f2, h1b[:], t1[:], ALU.add)
+        tt(e2, ab[:], u1[:], ALU.add)
         tt(t3, t2[:], b3, ALU.mult)
         tt(u3, u2[:], b3, ALU.mult)
         tt(t4, t3[:], q0b, ALU.add)
@@ -322,6 +335,14 @@ def tile_groupkanlayer_kernel(tc, x, W, b, p, q, out_0, out_1):
         tt(e0, u6[:], p0b, ALU.add)
 
         V5_LAG = 4
+
+        def last_product(k):
+            if ok(k - V5_LAG):
+                v5(k - V5_LAG)
+                if (k - V5_LAG) % C_TILES == C_TILES - 1 and (k - V5_LAG) // C_TILES < N_IDX - 1:
+                    jd = (k - V5_LAG) // C_TILES
+                    nc.sync.dma_start(out=hbm_view(out_0, jd), in_=ost[jd]["o0"][:])
+
         for k in range(-3, N_UNITS + V5_LAG + C_TILES + 1):
             if (k + 4) % 4 == 0 and 1 <= (k + 4) // 4 < N_IDX:
                 x_quantize((k + 4) // 4)
@@ -339,8 +360,10 @@ def tile_groupkanlayer_kernel(tc, x, W, b, p, q, out_0, out_1):
                 g2(k + 1)
             if ok(k - 1):
                 s2(k - 1)
-            if ok(k):
+            if ok(k) and not on_pool(k):
                 v3(k)
+            if ok(k) and on_pool(k):
+                last_product(k)
             if ok(k - 2):
                 t_r(k - 2)
             if (k + 6) % 4 == 0 and 1 <= (k + 6) // 4 < N_IDX:
@@ -348,7 +371,7 @@ def tile_groupkanlayer_kernel(tc, x, W, b, p, q, out_0, out_1):
             if (k + 5) % 4 == 0 and 1 <= (k + 5) // 4 < N_IDX:
                 x_copy((k + 5) // 4, 1)
             kc = k - V5_LAG - C_TILES
-            if 0 <= kc < N_UNITS:
+            if 0 <= kc < N_UNITS - C_TILES:
                 cast(kc // C_TILES, kc % C_TILES)
                 if kc % C_TILES == C_TILES - 1:
                     nc.sync.dma_start(out=hbm_view(out_1, kc // C_TILES), in_=ost[kc // C_TILES]["o1"][:].bitcast(U8))
@@ -358,8 +381,10 @@ def tile_groupkanlayer_kernel(tc, x, W, b, p, q, out_0, out_1):
                 s3(k - 1)
             if k >= 0 and k % 8 < 4 and k // 8 + 1 < G:
                 w_interleave(k // 8 + 1, k % 8)
-            if ok(k - 3):
+            if ok(k - 3) and k - 3 < 61:
                 t_n(k - 3)
+            if 61 <= k - 1 < N_UNITS:
+                t_n(k - 1)
             if ok(k):
                 v4(k)
             if ok(k - 3):
@@ -368,8 +393,5 @@ def tile_groupkanlayer_kernel(tc, x, W, b, p, q, out_0, out_1):
                 x_transpose((k + 7) // 4, 0)
             if (k + 6) % 4 == 0 and 1 <= (k + 6) // 4 < N_IDX:
                 x_transpose((k + 6) // 4, 1)
-            if ok(k - V5_LAG):
-                v5(k - V5_LAG)
-                if (k - V5_LAG) % C_TILES == C_TILES - 1:
-                    jd = (k - V5_LAG) // C_TILES
-                    nc.sync.dma_start(out=hbm_view(out_0, jd), in_=ost[jd]["o0"][:])
+            if not (ok(k) and on_pool(k)):
+                last_product(k)

@@ -244,23 +244,8 @@ def tile_groupkanlayer_kernel(tc, x, W, b, p, q, out_0, out_1):
             nc.scalar.activation(out=r_d[:].rearrange("p t n -> p (t n)"), in_=ust[u]["rb"][:].rearrange("p t n -> p (t n)"), func=ACT.Square)
             ust[u]["r_d"] = r_d
 
-        def hbm_unit_view(dram, u):
-            g, j, c = parts(u)
-            h = j % N_HALF
-            return dram[h * HALF : (h + 1) * HALF, g * GOUT + c * P : g * GOUT + (c + 1) * P].rearrange("(t p) n -> p t n", p=P)
-
         def v5(u):
             g, j, c = parts(u)
-            if j == N_IDX - 1:
-                o0u = outs.tile([P, T_IN_HALF, P], F32, name="o0u", bufs=4)
-                nc.vector.tensor_tensor(out=o0u[:], in0=ust[u]["r_d"][:], in1=ust[u]["nb"][:], op=ALU.mult)
-                nc.sync.dma_start(out=hbm_unit_view(out_0, u), in_=o0u[:])
-                o1u = outs.tile([P, T_IN_HALF, P], FP8, name="o1u", bufs=4)
-                nc.vector.tensor_scalar(
-                    out=o1u[:].rearrange("p t n -> p (t n)"), in0=o0u[:].rearrange("p t n -> p (t n)"), scalar1=Y_SCALE, scalar2=None, op0=ALU.mult, saturate=False
-                )
-                nc.sync.dma_start(out=hbm_unit_view(out_1, u), in_=o1u[:].bitcast(U8))
-                return
             if c == 0:
                 ost[j] = {"o0": outs.tile([P, T_IN_HALF, GOUT], F32, name="o0")}
             nc.vector.tensor_tensor(out=ost[j]["o0"][:, :, c * P : (c + 1) * P], in0=ust[u]["r_d"][:], in1=ust[u]["nb"][:], op=ALU.mult)
@@ -339,7 +324,7 @@ def tile_groupkanlayer_kernel(tc, x, W, b, p, q, out_0, out_1):
         def last_product(k):
             if ok(k - V5_LAG):
                 v5(k - V5_LAG)
-                if (k - V5_LAG) % C_TILES == C_TILES - 1 and (k - V5_LAG) // C_TILES < N_IDX - 1:
+                if (k - V5_LAG) % C_TILES == C_TILES - 1:
                     jd = (k - V5_LAG) // C_TILES
                     nc.sync.dma_start(out=hbm_view(out_0, jd), in_=ost[jd]["o0"][:])
 
@@ -371,7 +356,7 @@ def tile_groupkanlayer_kernel(tc, x, W, b, p, q, out_0, out_1):
             if (k + 5) % 4 == 0 and 1 <= (k + 5) // 4 < N_IDX:
                 x_copy((k + 5) // 4, 1)
             kc = k - V5_LAG - C_TILES
-            if 0 <= kc < N_UNITS - C_TILES:
+            if 0 <= kc < N_UNITS:
                 cast(kc // C_TILES, kc % C_TILES)
                 if kc % C_TILES == C_TILES - 1:
                     nc.sync.dma_start(out=hbm_view(out_1, kc // C_TILES), in_=ost[kc // C_TILES]["o1"][:].bitcast(U8))

@@ -129,7 +129,7 @@ def tile_groupkanlayer_kernel(tc, x, W, b, p, q, out_0, out_1):
         def x_copy(j, a):
             dst = xst[j]["grp"][:].bitcast(F32)[:, a * 512 : (a + 1) * 512].rearrange("p (t r u) -> p t r u", t=2, u=2)
             src = xst[j]["xt%d" % a][:].rearrange("p t u r -> p t r u")
-            if a == 1 and j % 2 == 1:
+            if a == 1 and j % 4 != 0:
                 nc.vector.tensor_copy(out=dst, in_=src)
             else:
                 nc.scalar.copy(out=dst, in_=src)
@@ -173,7 +173,7 @@ def tile_groupkanlayer_kernel(tc, x, W, b, p, q, out_0, out_1):
             return tile3[:, g, c : c + 1]
 
         def on_pool(u):
-            return u % 8 in (5, 7)
+            return u % 8 in (5, 6, 7)
 
         def g1(u):
             g = parts(u)[0]

@@ -324,8 +324,12 @@ def tile_groupkanlayer_kernel(tc, x, W, b, p, q, out_0, out_1):
         def last_product(k):
             if ok(k - V5_LAG):
                 v5(k - V5_LAG)
-                if (k - V5_LAG) % C_TILES == C_TILES - 1:
-                    jd = (k - V5_LAG) // C_TILES
+                u = k - V5_LAG
+                jd = u // C_TILES
+                if jd == N_IDX - 1 and u % 2 == 1:
+                    cs = slice((u % C_TILES - 1) * P, (u % C_TILES + 1) * P)
+                    nc.sync.dma_start(out=hbm_view(out_0, jd)[:, :, cs], in_=ost[jd]["o0"][:, :, cs])
+                elif jd < N_IDX - 1 and u % C_TILES == C_TILES - 1:
                     nc.sync.dma_start(out=hbm_view(out_0, jd), in_=ost[jd]["o0"][:])
 
         for k in range(-3, N_UNITS + V5_LAG + C_TILES + 1):

@@ -97,14 +97,7 @@ def tile_groupkanlayer_kernel(tc, x, W, b, p, q, out_0, out_1):
             if piece == 0:
                 wst[g] = {"grp": stage.tile([P, GOUT, 4], BF16, name="w_grp", align_bytes=64)}
             cs = slice(piece * P, (piece + 1) * P)
-            nc.gpsimd.tensor_scalar(
-                out=wst[g]["grp"][:, cs, :],
-                in0=w_raw[g][:, :, cs].rearrange("p j o -> p o j"),
-                scalar1=1.0,
-                scalar2=0.0,
-                op0=ALU.mult,
-                op1=ALU.add,
-            )
+            nc.gpsimd.tensor_copy(out=wst[g]["grp"][:, cs, :], in_=w_raw[g][:, :, cs].rearrange("p j o -> p o j"))
 
         def w_quantize(g):
             wc = stage.tile([P, GOUT], U32, name="w_codes", align_bytes=64)

@@ -122,7 +122,7 @@ def tile_groupkanlayer_kernel(tc, x, W, b, p, q, out_0, out_1):
         def x_copy(j, a):
             dst = xst[j]["grp"][:].bitcast(F32)[:, a * 512 : (a + 1) * 512].rearrange("p (t r u) -> p t r u", t=2, u=2)
             src = xst[j]["xt%d" % a][:].rearrange("p t u r -> p t r u")
-            if a == 1 and j % 4 != 0:
+            if j % 2 == 1 and j != 1:
                 nc.vector.tensor_copy(out=dst, in_=src)
             else:
                 nc.scalar.copy(out=dst, in_=src)

from contextlib import ExitStack

import concourse.masks as masks
import concourse.mybir as mybir

N_TOK, G, GIN, GOUT = 1024, 8, 512, 512
FLOPS = 2 * N_TOK * G * GIN * GOUT
Y_SCALE = 310.0

F32 = mybir.dt.float32
BF16 = mybir.dt.bfloat16
U32 = mybir.dt.uint32
U8 = mybir.dt.uint8
FP8X4 = mybir.dt.float8_e4m3fn_x4
FP8 = mybir.dt.float8_e4m3fn
ACT = mybir.ActivationFunctionType
ALU = mybir.AluOpType

P = 128
HALF = 512
N_HALF = N_TOK // HALF
T_IN_HALF = HALF // P
C_TILES = GOUT // P
N_IDX = G * N_HALF
N_UNITS = N_IDX * C_TILES


def tile_groupkanlayer_kernel(tc, x, W, b, p, q, out_0, out_1):
    nc = tc.nc
    with ExitStack() as ctx:
        const = ctx.enter_context(tc.tile_pool(name="const", bufs=1))
        raw = ctx.enter_context(tc.tile_pool(name="raw", bufs=1))
        stage = ctx.enter_context(tc.tile_pool(name="stage", bufs=2))
        work = ctx.enter_context(tc.tile_pool(name="work", bufs=3))
        outs = ctx.enter_context(tc.tile_pool(name="outs", bufs=3))
        ps_x = ctx.enter_context(tc.psum_pool(name="ps_x", bufs=1))
        ps_acc = ctx.enter_context(tc.psum_pool(name="ps_acc", bufs=3))
        ps_n = ctx.enter_context(tc.psum_pool(name="ps_n", bufs=2))
        ps_r = ctx.enter_context(tc.psum_pool(name="ps_r", bufs=2))
        ctx.enter_context(tc.manual_schedule())

        ident = const.tile([P, P], F32, name="ident")
        masks.make_identity(nc, ident[:])

        b_rows = const.tile([P, P], BF16, name="b_rows")
        nc.vector.memset(b_rows[:], 0.0)
        nc.scalar.dma_start(out=b_rows[0 : G * C_TILES, :], in_=b.rearrange("g (c n) -> (g c) n", n=P))
        pq_bf = const.tile([P, 56], BF16, name="pq_bf")
        nc.scalar.dma_start(out=pq_bf[:, 0:32], in_=p.rearrange("g k -> (g k)").partition_broadcast(P))
        nc.scalar.dma_start(out=pq_bf[:, 32:56], in_=q.rearrange("g k -> (g k)").partition_broadcast(P))
        one_col = const.tile([P, 1], F32, name="one_col")
        nc.vector.memset(one_col[:], 1.0)
        warm = const.tile([P, 1], F32, name="warm")
        nc.scalar.activation(out=warm[:], in_=one_col[:], func=ACT.Abs_reciprocal_sqrt)

        w_raw = []
        x_raw = []
        for g in range(G):
            w_raw.append(raw.tile([P, 4, GOUT], BF16, name="w_raw%d" % g))
            for h in range(N_HALF):
                x_raw.append(raw.tile([P, T_IN_HALF, GIN], BF16, name="x_raw%d_%d" % (g, h)))

        def load_w(g):
            nc.sync.dma_start(out=w_raw[g][:], in_=W[g, :, :].rearrange("(p j) o -> p j o", j=4))

        def load_x(j):
            g, h = divmod(j, N_HALF)
            nc.sync.dma_start(
                out=x_raw[j][:],
                in_=x[h * HALF : (h + 1) * HALF, g * GIN : (g + 1) * GIN].rearrange("(t p) k -> p t k", p=P),
            )

        for a in range(2):
            nc.sync.dma_start(
                out=x_raw[0][:, 2 * a : 2 * a + 2, :],
                in_=x[2 * a * P : (2 * a + 2) * P, 0:GIN].rearrange("(t p) k -> p t k", p=P),
            )
        load_w(0)
        load_x(1)
        for g in range(1, G):
            load_w(g)
            load_x(2 * g)
            load_x(2 * g + 1)

        def pcol(g, i):
            return pq[:, 4 * g + i : 4 * g + i + 1]

        def qcol(g, i):
            return pq[:, 32 + 3 * g + i : 32 + 3 * g + i + 1]

        wst = {}
        xst = {}
        ust = {}
        ost = {}

        def w_interleave(g, piece):
            if piece == 0:
                wst[g] = {"grp": stage.tile([P, GOUT, 4], BF16, name="w_grp", align_bytes=64)}
            cs = slice(piece * P, (piece + 1) * P)
            nc.gpsimd.tensor_copy(out=wst[g]["grp"][:, cs, :], in_=w_raw[g][:, :, cs].rearrange("p j o -> p o j"))

        def w_quantize(g):
            wc = stage.tile([P, GOUT], U32, name="w_codes", align_bytes=64)
            ws = stage.tile([P, GOUT], U8, name="w_scales", align_bytes=64)
            nc.vector.quantize_mx(out=wc[:].bitcast(FP8X4), scales=ws[:], in_=wst[g]["grp"][:].rearrange("p o j -> p (o j)"))
            wst[g]["codes"] = wc
            wst[g]["scales"] = ws

        def x_transpose(j, a, borrow=False):
            if a == 0:
                xst[j] = {"grp": stage.tile([P, HALF * 4], BF16, name="x_grp", align_bytes=64)}
            xw = x_raw[j][:].bitcast(F32)
            if borrow:
                xt = ps_r.tile([P, 2, 2, P], F32, name="xt_borrowed", tag="rb")
            else:
                xt = ps_x.tile([P, 2, 2, P], F32, name="xt", tag="xt")
            for tt in range(2):
                for u in range(2):
                    nc.tensor.transpose(out=xt[:, tt, u, :], in_=xw[:, 2 * a + tt, u : GIN // 2 : 2], identity=ident[:])
            xst[j]["xt%d" % a] = xt

        def x_copy(j, a):
            dst = xst[j]["grp"][:].bitcast(F32)[:, a * 512 : (a + 1) * 512].rearrange("p (t r u) -> p t r u", t=2, u=2)
            src = xst[j]["xt%d" % a][:].rearrange("p t u r -> p t r u")
            if j % 2 == 1 and j != 1:
                nc.vector.tensor_copy(out=dst, in_=src)
            else:
                nc.scalar.copy(out=dst, in_=src)

        def x_quantize(j):
            xc = stage.tile([P, HALF], U32, name="x_codes", align_bytes=64)
            xs = stage.tile([P, HALF], U8, name="x_scales", align_bytes=64)
            nc.vector.quantize_mx(out=xc[:].bitcast(FP8X4), scales=xs[:], in_=xst[j]["grp"][:])
            xst[j]["codes"] = xc
            xst[j]["scales"] = xs

        def ok(u):
            return 0 <= u < N_UNITS

        def parts(u):
            j, c = divmod(u, C_TILES)
            return j // N_HALF, j, c

        def mm(u):
            g, j, c = parts(u)
            cs = slice(c * P, (c + 1) * P)
            acc = ps_acc.tile([P, HALF], F32, name="acc", tag="acc")
            nc.tensor.matmul_mx(
                out=acc[:],
                lhsT=wst[g]["codes"][:, cs].bitcast(FP8X4),
                lhsT_scale=wst[g]["scales"][:, cs],
                rhs=xst[j]["codes"][:].bitcast(FP8X4),
                rhs_scale=xst[j]["scales"][:],
                start=True,
                stop=True,
            )
            ust[u] = {"acc": acc}

        def s1(u):
            s_t = work.tile([P, HALF], F32, name="s_t")
            nc.scalar.copy(out=s_t[:], in_=ust[u]["acc"][:])
            ust[u]["s_t"] = s_t

        def chan(tile3, u):
            g, j, c = parts(u)
            return tile3[:, g, c : c + 1]

        def on_pool(u):
            return u % 8 in (5, 6, 7)

        def g1(u):
            g = parts(u)[0]
            h1 = work.tile([P, HALF], F32, name="h1")
            nc.gpsimd.tensor_scalar(out=h1[:], in0=ust[u]["s_t"][:], scalar1=qcol(g, 2), scalar2=chan(f2, u), op0=ALU.mult, op1=ALU.add)
            ust[u]["h1"] = h1

        def g2(u):
            g = parts(u)[0]
            a_c = work.tile([P, HALF], F32, name="a_c")
            nc.gpsimd.tensor_scalar(out=a_c[:], in0=ust[u]["s_t"][:], scalar1=pcol(g, 3), scalar2=chan(e2, u), op0=ALU.mult, op1=ALU.add)
            ust[u]["a_c"] = a_c
            if on_pool(u):
                bb = work.tile([P, HALF], F32, name="bb")
                nc.gpsimd.tensor_tensor(out=bb[:], in0=a_c[:], in1=ust[u]["s_t"][:], op=ALU.mult)
                ust[u]["bb"] = bb

        def v1(u):
            h2 = work.tile([P, HALF], F32, name="h2")
            nc.vector.tensor_tensor(out=h2[:], in0=ust[u]["h1"][:], in1=ust[u]["acc"][:], op=ALU.mult)
            ust[u]["h2"] = h2

        def v2(u):
            h3 = work.tile([P, HALF], F32, name="h3")
            nc.vector.scalar_tensor_tensor(out=h3[:], in0=ust[u]["h2"][:], scalar=chan(f1, u), in1=ust[u]["acc"][:], op0=ALU.add, op1=ALU.mult)
            ust[u]["h3"] = h3

        def v3(u):
            if on_pool(u):
                return
            bb = work.tile([P, HALF], F32, name="bb")
            nc.vector.tensor_tensor(out=bb[:], in0=ust[u]["a_c"][:], in1=ust[u]["acc"][:], op=ALU.mult)
            ust[u]["bb"] = bb

        def v4(u):
            c_t = work.tile([P, HALF], F32, name="c_t", bufs=5)
            nc.vector.scalar_tensor_tensor(out=c_t[:], in0=ust[u]["bb"][:], scalar=chan(e1, u), in1=ust[u]["acc"][:], op0=ALU.add, op1=ALU.mult)
            ust[u]["c_t"] = c_t

        def s2(u):
            af_t = work.tile([P, HALF], F32, name="af_t")
            nc.scalar.activation(out=af_t[:], in_=ust[u]["h3"][:], func=ACT.Abs, bias=chan(f0, u), scale=1.0)
            ust[u]["af_t"] = af_t

        def s3(u):
            rs_t = work.tile([P, HALF], F32, name="rs_t")
            nc.scalar.activation(out=rs_t[:], in_=ust[u]["af_t"][:], func=ACT.Abs_reciprocal_sqrt, bias=one_col[:, 0:1], scale=1.0)
            ust[u]["rs_t"] = rs_t

        def t_r(u):
            rb = ps_r.tile([P, T_IN_HALF, P], F32, name="rb", tag="rb")
            for t in range(T_IN_HALF):
                nc.tensor.transpose(out=rb[:, t, :], in_=ust[u]["rs_t"][:, t * P : (t + 1) * P], identity=ident[:])
            ust[u]["rb"] = rb

        def t_n(u):
            if u >= 61:
                nb = ps_acc.tile([P, T_IN_HALF, P], F32, name="nb_borrowed", tag="acc")
            else:
                nb = ps_n.tile([P, T_IN_HALF, P], F32, name="nb")
            for t in range(T_IN_HALF):
                nc.tensor.matmul(out=nb[:, t, :], lhsT=chan(e0, u).to_broadcast([P, P]), rhs=ident[:], is_transpose=True, start=True, stop=False)
                nc.tensor.matmul(out=nb[:, t, :], lhsT=ust[u]["c_t"][:, t * P : (t + 1) * P], rhs=ident[:], is_transpose=True, start=False, stop=True)
            ust[u]["nb"] = nb

        def s4(u):
            r_d = work.tile([P, T_IN_HALF, P], F32, name="r_d")
            nc.scalar.activation(out=r_d[:].rearrange("p t n -> p (t n)"), in_=ust[u]["rb"][:].rearrange("p t n -> p (t n)"), func=ACT.Square)
            ust[u]["r_d"] = r_d

        def v5(u):
            g, j, c = parts(u)
            if c == 0:
                ost[j] = {"o0": outs.tile([P, T_IN_HALF, GOUT], F32, name="o0")}
            nc.vector.tensor_tensor(out=ost[j]["o0"][:, :, c * P : (c + 1) * P], in0=ust[u]["r_d"][:], in1=ust[u]["nb"][:], op=ALU.mult)

        def hbm_view(dram, j):
            g, h = divmod(j, N_HALF)
            return dram[h * HALF : (h + 1) * HALF, g * GOUT : (g + 1) * GOUT].rearrange("(t p) n -> p t n", p=P)

        def cast(j, t):
            if t == 0:
                ost[j]["o1"] = outs.tile([P, T_IN_HALF, GOUT], FP8, name="o1")
            if j >= 14:
                nc.vector.tensor_scalar(out=ost[j]["o1"][:, t, :], in0=ost[j]["o0"][:, t, :], scalar1=Y_SCALE, scalar2=None, op0=ALU.mult, saturate=False)
            else:
                nc.scalar.activation(out=ost[j]["o1"][:, t, :], in_=ost[j]["o0"][:, t, :], func=ACT.Copy, scale=Y_SCALE, saturate=False)

        x_transpose(0, 0)
        x_transpose(0, 1, borrow=True)
        x_copy(0, 0)
        x_copy(0, 1)
        wst[0] = {"grp": stage.tile([P, GOUT, 4], BF16, name="w_grp", align_bytes=64)}
        nc.vector.tensor_copy(out=wst[0]["grp"][:], in_=w_raw[0][:].rearrange("p j o -> p o j"))
        x_quantize(0)
        w_quantize(0)
        b_rows32 = const.tile([P, P], F32, name="b_rows32")
        nc.scalar.copy(out=b_rows32[:], in_=b_rows[:])
        b_ps = ps_x.tile([P, P], F32, name="b_ps", tag="xt")
        nc.tensor.transpose(out=b_ps[:], in_=b_rows32[:], identity=ident[:])
        b_col = const.tile([P, G * C_TILES], F32, name="b_col")
        nc.scalar.copy(out=b_col[:], in_=b_ps[:, 0 : G * C_TILES])
        pq = const.tile([P, 56], F32, name="pq")
        nc.scalar.copy(out=pq[:], in_=pq_bf[:])

        b3 = b_col[:].rearrange("p (g c) -> p g c", c=C_TILES)
        qv = pq[:, 32:56].rearrange("p (g k) -> p g k", k=3)
        q0b = qv[:, :, 0:1].to_broadcast([P, G, C_TILES])
        q1b = qv[:, :, 1:2].to_broadcast([P, G, C_TILES])
        q2b = qv[:, :, 2:3].to_broadcast([P, G, C_TILES])
        pv = pq[:, 0:32].rearrange("p (g k) -> p g k", k=4)
        p0b = pv[:, :, 0:1].to_broadcast([P, G, C_TILES])
        p1b = pv[:, :, 1:2].to_broadcast([P, G, C_TILES])
        p2b = pv[:, :, 2:3].to_broadcast([P, G, C_TILES])
        p3b = pv[:, :, 3:4].to_broadcast([P, G, C_TILES])

        def ctile(name):
            return const.tile([P, G, C_TILES], F32, name=name)

        def tt(out, in0, in1, op):
            nc.vector.tensor_tensor(out=out[:], in0=in0, in1=in1, op=op)

        t1, u1, h1b, ab, t2, u2, t3, u3 = ctile("t1"), ctile("u1"), ctile("h1b"), ctile("ab"), ctile("t2"), ctile("u2"), ctile("t3"), ctile("u3")
        f2, e2 = ctile("f2"), ctile("e2")
        t4, u4, f0, u6, t5, u5, f1, e1, e0 = ctile("t4"), ctile("u4"), ctile("f0"), ctile("u6"), ctile("t5"), ctile("u5"), ctile("f1"), ctile("e1"), ctile("e0")
        tt(t1, b3, q2b, ALU.mult)
        tt(u1, b3, p3b, ALU.mult)
        nc.vector.scalar_tensor_tensor(out=h1b[:], in0=t1[:], scalar=2.0, in1=q1b, op0=ALU.mult, op1=ALU.add)
        nc.vector.scalar_tensor_tensor(out=ab[:], in0=u1[:], scalar=2.0, in1=p2b, op0=ALU.mult, op1=ALU.add)
        tt(t2, t1[:], q1b, ALU.add)
        tt(u2, u1[:], p2b, ALU.add)
        tt(f2, h1b[:], t1[:], ALU.add)
        tt(e2, ab[:], u1[:], ALU.add)
        tt(t3, t2[:], b3, ALU.mult)
        tt(u3, u2[:], b3, ALU.mult)
        tt(t4, t3[:], q0b, ALU.add)
        tt(u4, u3[:], p1b, ALU.add)
        tt(f0, t4[:], b3, ALU.mult)
        tt(u6, u4[:], b3, ALU.mult)
        tt(t5, h1b[:], b3, ALU.mult)
        tt(u5, ab[:], b3, ALU.mult)
        tt(f1, t5[:], t4[:], ALU.add)
        tt(e1, u5[:], u4[:], ALU.add)
        tt(e0, u6[:], p0b, ALU.add)

        V5_LAG = 4

        def last_product(k):
            if ok(k - V5_LAG):
                v5(k - V5_LAG)
                u = k - V5_LAG
                jd = u // C_TILES
                if jd == N_IDX - 1 and u % 2 == 1:
                    cs = slice((u % C_TILES - 1) * P, (u % C_TILES + 1) * P)
                    nc.sync.dma_start(out=hbm_view(out_0, jd)[:, :, cs], in_=ost[jd]["o0"][:, :, cs])
                elif jd < N_IDX - 1 and u % C_TILES == C_TILES - 1:
                    nc.sync.dma_start(out=hbm_view(out_0, jd), in_=ost[jd]["o0"][:])

        for k in range(-3, N_UNITS + V5_LAG + C_TILES + 1):
            if (k + 4) % 4 == 0 and 1 <= (k + 4) // 4 < N_IDX:
                x_quantize((k + 4) // 4)
            if k >= 0 and k % 8 == 5 and k // 8 + 1 < G:
                w_quantize(k // 8 + 1)
            if ok(k + 1):
                s1(k + 1)
            if ok(k + 2):
                mm(k + 2)
            if ok(k):
                v1(k)
            if ok(k + 1):
                g1(k + 1)
            if ok(k + 1):
                g2(k + 1)
            if ok(k - 1):
                s2(k - 1)
            if ok(k) and not on_pool(k):
                v3(k)
            if ok(k) and on_pool(k):
                last_product(k)
            if ok(k - 2):
                t_r(k - 2)
            if (k + 6) % 4 == 0 and 1 <= (k + 6) // 4 < N_IDX:
                x_copy((k + 6) // 4, 0)
            if (k + 5) % 4 == 0 and 1 <= (k + 5) // 4 < N_IDX:
                x_copy((k + 5) // 4, 1)
            kc = k - V5_LAG - C_TILES
            if 0 <= kc < N_UNITS:
                cast(kc // C_TILES, kc % C_TILES)
                if kc % C_TILES == C_TILES - 1:
                    nc.sync.dma_start(out=hbm_view(out_1, kc // C_TILES), in_=ost[kc // C_TILES]["o1"][:].bitcast(U8))
            if ok(k):
                v2(k)
            if ok(k - 1):
                s3(k - 1)
            if k >= 0 and k % 8 < 4 and k // 8 + 1 < G:
                w_interleave(k // 8 + 1, k % 8)
            if ok(k - 3) and k - 3 < 61:
                t_n(k - 3)
            if 61 <= k - 1 < N_UNITS:
                t_n(k - 1)
            if ok(k):
                v4(k)
            if ok(k - 3):
                s4(k - 3)
            if (k + 7) % 4 == 0 and 1 <= (k + 7) // 4 < N_IDX:
                x_transpose((k + 7) // 4, 0)
            if (k + 6) % 4 == 0 and 1 <= (k + 6) // 4 < N_IDX:
                x_transpose((k + 6) // 4, 1)
            if not (ok(k) and on_pool(k)):
                last_product(k)
